import numpy as np
import ml_dtypes


def mxq(x, axis, fmt="e4m3"):
    dtype, down = {"e4m3": (ml_dtypes.float8_e4m3fn, 7), "e5m2": (ml_dtypes.float8_e5m2, 14)}[fmt]
    v = np.moveaxis(np.asarray(x, np.float32).astype(ml_dtypes.bfloat16).astype(np.float64), axis, -1)
    blocks = v.reshape(v.shape[:-1] + (-1, 32))
    amax = np.abs(blocks).max(-1, keepdims=True)
    byte = np.maximum(np.where(amax > 0, np.frexp(amax)[1] - 1 + 127, 0) - down, 1)
    scale = np.exp2(byte - 127.0)
    codes = (blocks / scale).astype(np.float32).astype(dtype).astype(np.float64)
    return np.moveaxis((codes * scale).reshape(v.shape), -1, axis)


WIDE = False


def mx_kscale(k):
    if not WIDE:
        return np.ones(k)
    levels = np.array([10, -10, 5, -5, 0])
    if k % 512:
        return np.exp2(np.random.permutation(np.resize(levels, k // 32))).repeat(32)
    a = np.empty((k // 512, 16))
    for p in range(k // 512):
        a[p, :8] = np.random.permutation(np.resize(levels, 8))
        for g in range(8):
            far = levels[np.abs(levels - a[p, g]) >= 10]
            a[p, g + 8] = far[np.random.randint(len(far))]
    return np.exp2(a.ravel()).repeat(32)


BF16 = ml_dtypes.bfloat16


def bf(x):
    return np.asarray(x, np.float32).astype(BF16)


def f64(x):
    return np.asarray(x).astype(np.float64)


B, T, C, H, KV, D = 2, 256, 2048, 16, 4, 128
EPS = 1e-5
THETA = 10000.0


def rmsnorm(h, w):
    var = np.mean(np.square(h), axis=-1, keepdims=True)
    return h * (1.0 / np.sqrt(var + EPS)) * w


def rope(h, cos, sin):
    hr = h.reshape(*h.shape[:-1], D // 2, 2)
    a, b = hr[..., 0], hr[..., 1]
    c = cos[None, :, None, :]
    s = sin[None, :, None, :]
    return np.stack([a * c - b * s, a * s + b * c], axis=-1).reshape(h.shape)


def draw0():
    s = mx_kscale(C)
    w_scale = 1.0 / np.sqrt(C)
    inv_freq = 1.0 / (THETA ** (np.arange(0, D, 2) / D))
    angles = np.arange(T)[:, None] * inv_freq[None, :]
    return {"x": bf(np.random.standard_normal((B, T, C)) * s),
            "Wq": bf(np.random.standard_normal((C, H * D)) * w_scale / s[:, None]),
            "bq": bf(np.random.standard_normal(H * D) * 0.1),
            "Wk": bf(np.random.standard_normal((C, KV * D)) * w_scale / s[:, None]),
            "bk": bf(np.random.standard_normal(KV * D) * 0.1),
            "Wv": bf(np.random.standard_normal((C, KV * D)) * w_scale / s[:, None]),
            "bv": bf(np.random.standard_normal(KV * D) * 0.1),
            "qn_w": bf(1.0 + 0.1 * np.random.standard_normal(D)),
            "kn_w": bf(1.0 + 0.1 * np.random.standard_normal(D)),
            "freqs_cos": bf(np.cos(angles)),
            "freqs_sin": bf(np.sin(angles))}


def core(x, Wq, bq, Wk, bk, Wv, bv, qn_w, kn_w, freqs_cos, freqs_sin):
    xq = mxq(f64(x), 2, "e4m3")
    q = ((xq @ mxq(f64(Wq), 0, "e4m3")) + f64(bq)).reshape(B, T, H, D)
    k = ((xq @ mxq(f64(Wk), 0, "e4m3")) + f64(bk)).reshape(B, T, KV, D)
    v = ((xq @ mxq(f64(Wv), 0, "e4m3")) + f64(bv)).reshape(B, T, KV, D)
    q = rmsnorm(q, f64(qn_w))
    k = rmsnorm(k, f64(kn_w))
    q = rope(q, f64(freqs_cos), f64(freqs_sin))
    k = rope(k, f64(freqs_cos), f64(freqs_sin))
    return q, k, v


def e4m3fn_bytes(y):
    return np.clip(np.asarray(y, np.float64), -448.0, 448.0).astype(np.float32).astype(ml_dtypes.float8_e4m3fn).view(np.uint8)


def e4m3fn_values(b):
    return np.asarray(b, np.uint8).view(ml_dtypes.float8_e4m3fn).astype(np.float64)


def setup_inputs():
    d = draw0()
    x0 = np.asarray(d['Wq']).astype(np.float64)
    s = (np.max(np.abs(x0), axis=(1,), keepdims=True) / 448.0).astype(np.float32)
    out = {}
    for k, v in d.items():
        if k == 'Wq':
            out['Wq_bytes'] = e4m3fn_bytes(x0 / s.astype(np.float64))
            out['Wq_scale'] = s
        else:
            out[k] = v
    return out


def reference(x, Wq_bytes, Wq_scale, bq, Wk, bk, Wv, bv, qn_w, kn_w, freqs_cos, freqs_sin):
    return core(x, e4m3fn_values(Wq_bytes) * Wq_scale.astype(np.float64), bq, Wk, bk, Wv, bv, qn_w, kn_w, freqs_cos, freqs_sin)

@@ -1,0 +1,324 @@
+from contextlib import ExitStack
+
+import concourse.mybir as mybir
+from concourse.masks import make_identity
+
+B, T, C, H, KV, D = 2, 256, 2048, 16, 4, 128
+EPS = 1e-5
+FLOPS = 2 * (B * T) * C * (H + 2 * KV) * D
+
+F32 = mybir.dt.float32
+BF16 = mybir.dt.bfloat16
+U32 = mybir.dt.uint32
+U8 = mybir.dt.uint8
+FP8 = mybir.dt.float8_e4m3fn
+FP8X4 = mybir.dt.float8_e4m3fn_x4
+ALU = mybir.AluOpType
+ACT = mybir.ActivationFunctionType
+
+P = 128
+PACK = 4
+PASSES = C // (P * PACK)
+TOK_TILES = (B * T) // P
+CHUNK = 512
+HEADS = CHUNK // D
+
+CHUNKS = (("q", 0), ("q", 1), ("q", 2), ("q", 3), ("k", 0), ("v", 0))
+UNITS = len(CHUNKS) * PASSES
+TILES = len(CHUNKS) * TOK_TILES
+EPI_LAG = 5
+
+PLANES_ON_SCALAR = (3, 4, 4, 4, 0, 0)
+COLS_ON_SCALAR = (0, 192, 192, 192, 512, 512)
+
+
+def tile_llamacausalselfattention_pa_kernel(
+    tc, x, Wq_bytes, Wq_scale, bq, Wk, bk, Wv, bv, qn_w, kn_w, freqs_cos, freqs_sin, out_0, out_1, out_2
+):
+    nc = tc.nc
+    with ExitStack() as ctx:
+        ctx.enter_context(tc.manual_schedule())
+        const = ctx.enter_context(tc.tile_pool(name="const", bufs=1))
+        raw = ctx.enter_context(tc.tile_pool(name="raw", bufs=1))
+        prep = ctx.enter_context(tc.tile_pool(name="prep", bufs=3))
+        epi = ctx.enter_context(tc.tile_pool(name="epi", bufs=3))
+        psum = ctx.enter_context(tc.psum_pool(name="psum", bufs=8))
+
+        xv = x.rearrange("b t c -> (b t) c")
+        wqv = Wq_bytes.rearrange("(g p t) n -> g p t n", p=P, t=PACK)
+        wkv = Wk.rearrange("(g p t) n -> g p t n", p=P, t=PACK)
+        wvv = Wv.rearrange("(g p t) n -> g p t n", p=P, t=PACK)
+        outs = {
+            "q": out_0.rearrange("b t h d -> (b t) (h d)"),
+            "k": out_1.rearrange("b t h d -> (b t) (h d)"),
+            "v": out_2.rearrange("b t h d -> (b t) (h d)"),
+        }
+
+        wsc = const.tile([P, PASSES, PACK], F32, name="wsc")
+        nc.scalar.dma_start(out=wsc[:], in_=Wq_scale.rearrange("(g p t) o -> p g (t o)", p=P, t=PACK))
+        cos = const.tile([P, 2, D // 2], BF16, name="cos")
+        nc.scalar.dma_start(out=cos[:], in_=freqs_cos.rearrange("(i p) j -> p i j", p=P))
+        sin = const.tile([P, 2, D // 2], BF16, name="sin")
+        nc.scalar.dma_start(out=sin[:], in_=freqs_sin.rearrange("(i p) j -> p i j", p=P))
+        gain = {}
+        for kind, vec in (("q", qn_w), ("k", kn_w)):
+            gain[kind] = const.tile([P, D], BF16, name="gain_" + kind)
+            nc.scalar.dma_start(out=gain[kind][:], in_=vec.partition_broadcast(P))
+
+        bias = const.tile([P, len(CHUNKS) * CHUNK], BF16, name="bias")
+
+        def load_bias(c):
+            kind, cq = CHUNKS[c]
+            vec = {"q": bq, "k": bk, "v": bv}[kind]
+            nc.sync.dma_start(
+                out=bias[:, c * CHUNK : (c + 1) * CHUNK],
+                in_=vec[cq * CHUNK : (cq + 1) * CHUNK].partition_broadcast(P),
+            )
+
+        wq8a = []
+        wq8b = []
+        xraw = []
+        wkraw = []
+        wvraw = []
+        for g in range(PASSES):
+            wq8a.append(raw.tile([P, PACK, CHUNK], U8, name="wq8a%d" % g))
+            nc.sync.dma_start(out=wq8a[g][:], in_=wqv[g][:, :, 0:CHUNK])
+        for i in range(TOK_TILES):
+            xraw.append(raw.tile([P, C], BF16, name="xraw%d" % i))
+            nc.sync.dma_start(out=xraw[i][:], in_=xv[i * P : (i + 1) * P, :])
+        load_bias(0)
+        for g in range(PASSES):
+            wq8b.append(raw.tile([P, PACK, 3 * CHUNK], U8, name="wq8b%d" % g))
+            nc.sync.dma_start(out=wq8b[g][:], in_=wqv[g][:, :, CHUNK : 4 * CHUNK])
+            if g == 1:
+                load_bias(1)
+        load_bias(2)
+        load_bias(3)
+        for g in range(PASSES):
+            wkraw.append(raw.tile([P, PACK, CHUNK], BF16, name="wkraw%d" % g))
+            nc.sync.dma_start(out=wkraw[g][:], in_=wkv[g])
+        load_bias(4)
+        for g in range(PASSES):
+            wvraw.append(raw.tile([P, PACK, CHUNK], BF16, name="wvraw%d" % g))
+            nc.sync.dma_start(out=wvraw[g][:], in_=wvv[g])
+        load_bias(5)
+
+        zero = const.tile([P, 1], F32, name="zero")
+        nc.vector.memset(zero[:], 0.0)
+        eps = const.tile([P, 1], F32, name="eps")
+        nc.vector.tensor_scalar(out=eps[:], in0=zero[:], scalar1=1.0, scalar2=EPS, op0=ALU.mult, op1=ALU.add)
+        warm = const.tile([P, 1], F32, name="warm")
+        nc.scalar.activation(out=warm[:], in_=eps[:], func=ACT.Sqrt)
+        ident = const.tile([P, P], F32, name="ident")
+        make_identity(nc, ident[:])
+
+        ssin = const.tile([P, 2, D // 2, 2], BF16, name="ssin")
+        nc.gpsimd.tensor_copy(out=ssin[:, :, :, 0], in_=sin[:])
+        nc.gpsimd.tensor_scalar(out=ssin[:, :, :, 1], in0=sin[:], scalar1=-1.0, scalar2=0.0, op0=ALU.mult, op1=ALU.add)
+        table = {}
+        for kind in ("q", "k"):
+            for i in range(2):
+                tab = const.tile([P, 2, D], F32, name="table_%s%d" % (kind, i))
+                pairs = gain[kind][:].rearrange("p (j e) -> p j e", e=2)
+                nc.gpsimd.tensor_tensor(
+                    out=tab[:, 0, :].rearrange("p (j e) -> p j e", e=2),
+                    in0=pairs,
+                    in1=cos[:, i, :].unsqueeze(2).to_broadcast([P, D // 2, 2]),
+                    op=ALU.mult,
+                )
+                nc.gpsimd.tensor_tensor(
+                    out=tab[:, 1, :].rearrange("p (j e) -> p j e", e=2),
+                    in0=pairs,
+                    in1=ssin[:, i, :, :],
+                    op=ALU.mult,
+                )
+                table[(kind, i)] = tab
+
+        xgrouped = {}
+        xcodes = []
+        xscales = []
+        for i in range(TOK_TILES):
+            xcodes.append(const.tile([P, PASSES * P], U32, name="xcodes%d" % i, align_bytes=64))
+            xscales.append(const.tile([P, PASSES * P], U8, name="xscales%d" % i, align_bytes=64))
+
+        def turn_x(i):
+            words = xraw[i][:].bitcast(F32)
+            xg = prep.tile([P, PASSES * P * PACK], BF16, name="xg", tag="xg", bufs=2, align_bytes=64)
+            xgrouped[i] = xg
+            xg_words = xg[:].bitcast(F32).rearrange("p (g r u) -> p g r u", g=PASSES, u=2)
+            for half in range(PASSES // 2):
+                xt = psum.tile([P, 2, 2, P], F32, name="xt", tag="bank")
+                for gg in range(2):
+                    g = 2 * half + gg
+                    for u in range(2):
+                        nc.tensor.transpose(xt[:, gg, u, :], words[:, 256 * g + u : 256 * (g + 1) : 2], ident[:])
+                nc.scalar.copy(
+                    out=xg_words[:, 2 * half : 2 * half + 2, :, :],
+                    in_=xt[:].rearrange("p g u r -> p g r u"),
+                )
+
+        def quantize_x(i):
+            nc.vector.quantize_mx(out=xcodes[i][:].bitcast(FP8X4), scales=xscales[i][:], in_=xgrouped[i][:])
+
+        planes = {}
+        grouped = {}
+        wcodes = {}
+        wscales = {}
+
+        def widen(u, on_scalar):
+            c, g = divmod(u, PASSES)
+            kind, cq = CHUNKS[c]
+            if kind == "k":
+                planes[u] = wkraw[g]
+            if kind == "v":
+                planes[u] = wvraw[g]
+            if kind != "q":
+                return
+            if u not in planes:
+                planes[u] = prep.tile([P, PACK, CHUNK], BF16, name="wide", tag="wide")
+            src = wq8a[g] if cq == 0 else wq8b[g]
+            lo = 0 if cq == 0 else (cq - 1) * CHUNK
+            for t in range(PACK):
+                codes8 = src[:, t, lo : lo + CHUNK].bitcast(FP8)
+                scale = wsc[:, g, t : t + 1]
+                if on_scalar and t < PLANES_ON_SCALAR[c]:
+                    nc.scalar.activation(out=planes[u][:, t, :], in_=codes8, func=ACT.Copy, scale=scale)
+                if (not on_scalar) and t >= PLANES_ON_SCALAR[c]:
+                    nc.vector.tensor_scalar(out=planes[u][:, t, :], in0=codes8, scalar1=scale, scalar2=None, op0=ALU.mult)
+
+        def interleave(u):
+            c = u // PASSES
+            ns = COLS_ON_SCALAR[c]
+            gr = prep.tile([P, CHUNK, PACK], BF16, name="grouped", tag="grouped", align_bytes=64)
+            grouped[u] = gr
+            if ns > 0:
+                nc.scalar.copy(out=gr[:, 0:ns, :], in_=planes[u][:, :, 0:ns].rearrange("p t n -> p n t"))
+            if ns < CHUNK:
+                nc.vector.tensor_copy(out=gr[:, ns:CHUNK, :], in_=planes[u][:, :, ns:CHUNK].rearrange("p t n -> p n t"))
+
+        def quantize(u):
+            wcodes[u] = prep.tile([P, CHUNK], U32, name="wcodes", tag="wcodes", bufs=6, align_bytes=64)
+            wscales[u] = prep.tile([P, CHUNK], U8, name="wscales", tag="wscales", bufs=6, align_bytes=64)
+            nc.vector.quantize_mx(
+                out=wcodes[u][:].bitcast(FP8X4),
+                scales=wscales[u][:],
+                in_=grouped[u][:].rearrange("p n t -> p (n t)"),
+            )
+
+        acc = {}
+
+        def multiply(u, i):
+            c, g = divmod(u, PASSES)
+            e = c * TOK_TILES + i
+            if g == 0:
+                acc[e] = psum.tile([P, CHUNK], F32, name="acc", tag="bank")
+            nc.tensor.matmul_mx(
+                out=acc[e][:],
+                lhsT=xcodes[i][:, g * P : (g + 1) * P].bitcast(FP8X4),
+                lhsT_scale=xscales[i][:, g * P : (g + 1) * P],
+                rhs=wcodes[u][:].bitcast(FP8X4),
+                rhs_scale=wscales[u][:],
+                start=(g == 0),
+                stop=(g == PASSES - 1),
+            )
+
+        hb = {}
+        m1 = {}
+        rstd = {}
+        rms = {}
+
+        def store(e, res):
+            c, i = divmod(e, TOK_TILES)
+            kind, cq = CHUNKS[c]
+            nc.sync.dma_start(out=outs[kind][i * P : (i + 1) * P, cq * CHUNK : (cq + 1) * CHUNK], in_=res[:])
+
+        def normed(e):
+            return 0 <= e < TILES and CHUNKS[e // TOK_TILES][0] != "v"
+
+        def add_bias(e):
+            c = e // TOK_TILES
+            if normed(e):
+                hb[e] = epi.tile([P, CHUNK], F32, name="hb", tag="hb")
+            else:
+                hb[e] = epi.tile([P, CHUNK], F32, name="res", tag="res", bufs=4)
+            nc.vector.tensor_tensor(out=hb[e][:], in0=acc[e][:], in1=bias[:, c * CHUNK : (c + 1) * CHUNK], op=ALU.add)
+            if not normed(e):
+                store(e, hb[e])
+
+        def mean_square(e):
+            ss = epi.tile([P, HEADS], F32, name="ss", tag="ss", bufs=4)
+            for h in range(HEADS):
+                junk = epi.tile([P, D], F32, name="junk", tag="junk", bufs=2)
+                nc.scalar.activation(out=junk[:], in_=hb[e][:, h * D : (h + 1) * D], func=ACT.Square, accum_out=ss[:, h : h + 1])
+            rms[e] = epi.tile([P, HEADS], F32, name="rms", tag="rms", bufs=4)
+            nc.scalar.activation(out=rms[e][:], in_=ss[:], func=ACT.Sqrt, bias=eps[:], scale=1.0 / D)
+
+        def invert(e):
+            rstd[e] = epi.tile([P, HEADS], F32, name="rstd", tag="rstd", bufs=4)
+            nc.vector.reciprocal(out=rstd[e][:], in_=rms[e][:])
+
+        def tab_of(e):
+            c, i = divmod(e, TOK_TILES)
+            return table[(CHUNKS[c][0], i % 2)]
+
+        def rope_first(e):
+            m1[e] = epi.tile([P, CHUNK], F32, name="m1", tag="m1")
+            nc.vector.tensor_tensor(
+                out=m1[e][:].rearrange("p (h d) -> p h d", h=HEADS),
+                in0=hb[e][:].rearrange("p (h d) -> p h d", h=HEADS),
+                in1=tab_of(e)[:, 0, :].unsqueeze(1).to_broadcast([P, HEADS, D]),
+                op=ALU.mult,
+            )
+
+        def rope_rest(e):
+            m2 = epi.tile([P, CHUNK], F32, name="m2", tag="m2", bufs=2)
+            res = epi.tile([P, CHUNK], F32, name="res", tag="res", bufs=4)
+            for h in range(HEADS):
+                cols = slice(h * D, (h + 1) * D)
+                nc.vector.scalar_tensor_tensor(
+                    out=m2[:, cols], in0=hb[e][:, cols], scalar=rstd[e][:, h : h + 1], in1=tab_of(e)[:, 1, :],
+                    op0=ALU.mult, op1=ALU.mult,
+                )
+            for h in range(HEADS):
+                cols = slice(h * D, (h + 1) * D)
+                nc.vector.scalar_tensor_tensor(
+                    out=res[:, cols].rearrange("p (j e) -> p j e", e=2),
+                    in0=m1[e][:, cols].rearrange("p (j e) -> p j e", e=2),
+                    scalar=rstd[e][:, h : h + 1],
+                    in1=m2[:, cols].rearrange("p (j e) -> p j e", e=2)[:, :, ::-1],
+                    op0=ALU.mult, op1=ALU.add,
+                )
+            store(e, res)
+
+        widen(0, True)
+        widen(0, False)
+        for s in range(UNITS + EPI_LAG + 2):
+            e = s - EPI_LAG
+            if s + 1 < UNITS:
+                widen(s + 1, True)
+            if s < TOK_TILES:
+                turn_x(s)
+            if 1 <= s <= TOK_TILES:
+                quantize_x(s - 1)
+            if 1 <= s <= UNITS:
+                quantize(s - 1)
+            if s == PASSES:
+                for i in range(TOK_TILES):
+                    for g in range(PASSES):
+                        multiply(g, i)
+            if PASSES < s <= UNITS:
+                for i in range(TOK_TILES):
+                    multiply(s - 1, i)
+            if 0 <= e < TILES:
+                add_bias(e)
+            if normed(e - 1):
+                invert(e - 1)
+            if s + 1 < UNITS:
+                widen(s + 1, False)
+            if s < UNITS:
+                interleave(s)
+            if normed(e):
+                rope_first(e)
+                mean_square(e)
+            if normed(e - 1):
+                rope_rest(e - 1)

@@ -21,6 +21,7 @@ PACK = 4
 PASSES = C // (P * PACK)
 TOK_TILES = (B * T) // P
 CHUNK = 512
+HALF = CHUNK // 2
 HEADS = CHUNK // D
 
 CHUNKS = (("q", 0), ("q", 1), ("q", 2), ("q", 3), ("k", 0), ("v", 0))
@@ -28,8 +29,9 @@ UNITS = len(CHUNKS) * PASSES
 TILES = len(CHUNKS) * TOK_TILES
 EPI_LAG = 5
 
-PLANES_ON_SCALAR = (3, 4, 4, 4, 0, 0)
-COLS_ON_SCALAR = (0, 192, 192, 192, 512, 512)
+PLANES_ON_SCALAR = (3, 3, 3, 3, 0, 0)
+A_ON_GPSIMD = (False, True, True, True, True, True)
+B_COLS_ON_SCALAR = (0, 96, 96, 96, 256, 256)
 
 
 def tile_llamacausalselfattention_pa_kernel(
@@ -42,7 +44,7 @@ def tile_llamacausalselfattention_pa_kernel(
         raw = ctx.enter_context(tc.tile_pool(name="raw", bufs=1))
         prep = ctx.enter_context(tc.tile_pool(name="prep", bufs=3))
         epi = ctx.enter_context(tc.tile_pool(name="epi", bufs=3))
-        psum = ctx.enter_context(tc.psum_pool(name="psum", bufs=8))
+        psum = ctx.enter_context(tc.psum_pool(name="psum", bufs=6))
 
         xv = x.rearrange("b t c -> (b t) c")
         wqv = Wq_bytes.rearrange("(g p t) n -> g p t n", p=P, t=PACK)
@@ -108,31 +110,51 @@ def tile_llamacausalselfattention_pa_kernel(
         eps = const.tile([P, 1], F32, name="eps")
         nc.vector.tensor_scalar(out=eps[:], in0=zero[:], scalar1=1.0, scalar2=EPS, op0=ALU.mult, op1=ALU.add)
         warm = const.tile([P, 1], F32, name="warm")
-        nc.scalar.activation(out=warm[:], in_=eps[:], func=ACT.Sqrt)
+        nc.scalar.activation(out=warm[:], in_=eps[:], func=ACT.Abs_reciprocal_sqrt)
         ident = const.tile([P, P], F32, name="ident")
         make_identity(nc, ident[:])
 
         ssin = const.tile([P, 2, D // 2, 2], BF16, name="ssin")
         nc.gpsimd.tensor_copy(out=ssin[:, :, :, 0], in_=sin[:])
         nc.gpsimd.tensor_scalar(out=ssin[:, :, :, 1], in0=sin[:], scalar1=-1.0, scalar2=0.0, op0=ALU.mult, op1=ALU.add)
-        table = {}
-        for kind in ("q", "k"):
-            for i in range(2):
-                tab = const.tile([P, 2, D], F32, name="table_%s%d" % (kind, i))
+        KIND_ROW = {"q": 0, "k": 1}
+        table_sb = []
+        for i in range(2):
+            tab = const.tile([P, 2, 2, D], F32, name="table_sb%d" % i)
+            table_sb.append(tab)
+            for kind in ("q", "k"):
                 pairs = gain[kind][:].rearrange("p (j e) -> p j e", e=2)
                 nc.gpsimd.tensor_tensor(
-                    out=tab[:, 0, :].rearrange("p (j e) -> p j e", e=2),
+                    out=tab[:, KIND_ROW[kind], 0, :].rearrange("p (j e) -> p j e", e=2),
                     in0=pairs,
                     in1=cos[:, i, :].unsqueeze(2).to_broadcast([P, D // 2, 2]),
                     op=ALU.mult,
                 )
                 nc.gpsimd.tensor_tensor(
-                    out=tab[:, 1, :].rearrange("p (j e) -> p j e", e=2),
+                    out=tab[:, KIND_ROW[kind], 1, :].rearrange("p (j e) -> p j e", e=2),
                     in0=pairs,
                     in1=ssin[:, i, :, :],
                     op=ALU.mult,
                 )
-                table[(kind, i)] = tab
+
+        table_ps = []
+        table_turned = []
+
+        def turn_table(i):
+            turned_ps = psum.tile([P, 2, 2, D], F32, name="turned_ps", tag="bank")
+            for a in range(2):
+                for b in range(2):
+                    nc.tensor.transpose(turned_ps[:, a, b, :], table_sb[i][:, a, b, :], ident[:])
+            turned = const.tile([P, 2, 2, D], F32, name="turned%d" % i)
+            table_turned.append(turned)
+            nc.vector.tensor_copy(out=turned[:], in_=turned_ps[:])
+
+        def table_to_psum(i):
+            tab = psum.tile([P, 2, 2, D], F32, name="table_ps%d" % i, tag="table_ps%d" % i, bufs=1)
+            table_ps.append(tab)
+            for a in range(2):
+                for b in range(2):
+                    nc.tensor.transpose(tab[:, a, b, :], table_turned[i][:, a, b, :], ident[:])
 
         xgrouped = {}
         xcodes = []
@@ -161,7 +183,8 @@ def tile_llamacausalselfattention_pa_kernel(
             nc.vector.quantize_mx(out=xcodes[i][:].bitcast(FP8X4), scales=xscales[i][:], in_=xgrouped[i][:])
 
         planes = {}
-        grouped = {}
+        group_a = {}
+        group_b = {}
         wcodes = {}
         wscales = {}
 
@@ -186,24 +209,33 @@ def tile_llamacausalselfattention_pa_kernel(
                 if (not on_scalar) and t >= PLANES_ON_SCALAR[c]:
                     nc.vector.tensor_scalar(out=planes[u][:, t, :], in0=codes8, scalar1=scale, scalar2=None, op0=ALU.mult)
 
-        def interleave(u):
-            c = u // PASSES
-            ns = COLS_ON_SCALAR[c]
-            gr = prep.tile([P, CHUNK, PACK], BF16, name="grouped", tag="grouped", align_bytes=64)
-            grouped[u] = gr
+        def interleave_b(u):
+            ns = B_COLS_ON_SCALAR[u // PASSES]
+            gr = prep.tile([P, HALF, PACK], BF16, name="group_b", tag="group_b", align_bytes=64)
+            group_b[u] = gr
             if ns > 0:
-                nc.scalar.copy(out=gr[:, 0:ns, :], in_=planes[u][:, :, 0:ns].rearrange("p t n -> p n t"))
-            if ns < CHUNK:
-                nc.vector.tensor_copy(out=gr[:, ns:CHUNK, :], in_=planes[u][:, :, ns:CHUNK].rearrange("p t n -> p n t"))
+                nc.scalar.copy(out=gr[:, 0:ns, :], in_=planes[u][:, :, HALF : HALF + ns].rearrange("p t n -> p n t"))
+            if ns < HALF:
+                nc.vector.tensor_copy(out=gr[:, ns:HALF, :], in_=planes[u][:, :, HALF + ns : CHUNK].rearrange("p t n -> p n t"))
+
+        def interleave_a(u):
+            gr = prep.tile([P, HALF, PACK], BF16, name="group_a", tag="group_a", bufs=1, align_bytes=64)
+            group_a[u] = gr
+            turned = planes[u][:, :, 0:HALF].rearrange("p t n -> p n t")
+            if A_ON_GPSIMD[u // PASSES]:
+                nc.gpsimd.tensor_scalar(out=gr[:], in0=turned, scalar1=1.0, scalar2=0.0, op0=ALU.mult, op1=ALU.add)
+            else:
+                nc.vector.tensor_copy(out=gr[:], in_=turned)
 
         def quantize(u):
             wcodes[u] = prep.tile([P, CHUNK], U32, name="wcodes", tag="wcodes", bufs=6, align_bytes=64)
             wscales[u] = prep.tile([P, CHUNK], U8, name="wscales", tag="wscales", bufs=6, align_bytes=64)
-            nc.vector.quantize_mx(
-                out=wcodes[u][:].bitcast(FP8X4),
-                scales=wscales[u][:],
-                in_=grouped[u][:].rearrange("p n t -> p (n t)"),
-            )
+            for lo, gr in ((HALF, group_b[u]), (0, group_a[u])):
+                nc.vector.quantize_mx(
+                    out=wcodes[u][:, lo : lo + HALF].bitcast(FP8X4),
+                    scales=wscales[u][:, lo : lo + HALF],
+                    in_=gr[:].rearrange("p n t -> p (n t)"),
+                )
 
         acc = {}
 
@@ -223,9 +255,9 @@ def tile_llamacausalselfattention_pa_kernel(
             )
 
         hb = {}
-        m1 = {}
+        prod = {}
+        rot = {}
         rstd = {}
-        rms = {}
 
         def store(e, res):
             c, i = divmod(e, TOK_TILES)
@@ -250,75 +282,79 @@ def tile_llamacausalselfattention_pa_kernel(
             for h in range(HEADS):
                 junk = epi.tile([P, D], F32, name="junk", tag="junk", bufs=2)
                 nc.scalar.activation(out=junk[:], in_=hb[e][:, h * D : (h + 1) * D], func=ACT.Square, accum_out=ss[:, h : h + 1])
-            rms[e] = epi.tile([P, HEADS], F32, name="rms", tag="rms", bufs=4)
-            nc.scalar.activation(out=rms[e][:], in_=ss[:], func=ACT.Sqrt, bias=eps[:], scale=1.0 / D)
-
-        def invert(e):
             rstd[e] = epi.tile([P, HEADS], F32, name="rstd", tag="rstd", bufs=4)
-            nc.vector.reciprocal(out=rstd[e][:], in_=rms[e][:])
+            nc.scalar.activation(out=rstd[e][:], in_=ss[:], func=ACT.Abs_reciprocal_sqrt, bias=eps[:], scale=1.0 / D)
 
-        def tab_of(e):
+        def rope_products(e):
             c, i = divmod(e, TOK_TILES)
-            return table[(CHUNKS[c][0], i % 2)]
-
-        def rope_first(e):
-            m1[e] = epi.tile([P, CHUNK], F32, name="m1", tag="m1")
+            tab = table_ps[i % 2][:, KIND_ROW[CHUNKS[c][0]], :, :]
+            prod[e] = epi.tile([P, 2, HEADS, D], F32, name="prod", tag="prod")
             nc.vector.tensor_tensor(
-                out=m1[e][:].rearrange("p (h d) -> p h d", h=HEADS),
-                in0=hb[e][:].rearrange("p (h d) -> p h d", h=HEADS),
-                in1=tab_of(e)[:, 0, :].unsqueeze(1).to_broadcast([P, HEADS, D]),
+                out=prod[e][:],
+                in0=hb[e][:].rearrange("p (h d) -> p h d", h=HEADS).unsqueeze(1).to_broadcast([P, 2, HEADS, D]),
+                in1=tab.unsqueeze(2).to_broadcast([P, 2, HEADS, D]),
                 op=ALU.mult,
             )
 
-        def rope_rest(e):
-            m2 = epi.tile([P, CHUNK], F32, name="m2", tag="m2", bufs=2)
+        def rope_sum(e):
+            rot[e] = epi.tile([P, CHUNK], F32, name="rot", tag="rot")
+            nc.vector.tensor_tensor(
+                out=rot[e][:].rearrange("p (j e) -> p j e", e=2),
+                in0=prod[e][:, 0, :, :].rearrange("p h (j e) -> p (h j) e", e=2),
+                in1=prod[e][:, 1, :, :].rearrange("p h (j e) -> p (h j) e", e=2)[:, :, ::-1],
+                op=ALU.add,
+            )
+
+        def scale_out(e):
             res = epi.tile([P, CHUNK], F32, name="res", tag="res", bufs=4)
             for h in range(HEADS):
                 cols = slice(h * D, (h + 1) * D)
-                nc.vector.scalar_tensor_tensor(
-                    out=m2[:, cols], in0=hb[e][:, cols], scalar=rstd[e][:, h : h + 1], in1=tab_of(e)[:, 1, :],
-                    op0=ALU.mult, op1=ALU.mult,
-                )
-            for h in range(HEADS):
-                cols = slice(h * D, (h + 1) * D)
-                nc.vector.scalar_tensor_tensor(
-                    out=res[:, cols].rearrange("p (j e) -> p j e", e=2),
-                    in0=m1[e][:, cols].rearrange("p (j e) -> p j e", e=2),
-                    scalar=rstd[e][:, h : h + 1],
-                    in1=m2[:, cols].rearrange("p (j e) -> p j e", e=2)[:, :, ::-1],
-                    op0=ALU.mult, op1=ALU.add,
-                )
+                nc.scalar.activation(out=res[:, cols], in_=rot[e][:, cols], func=ACT.Copy, scale=rstd[e][:, h : h + 1])
             store(e, res)
 
+        late = []
         widen(0, True)
         widen(0, False)
-        for s in range(UNITS + EPI_LAG + 2):
+        for s in range(UNITS + EPI_LAG):
             e = s - EPI_LAG
             if s + 1 < UNITS:
                 widen(s + 1, True)
             if s < TOK_TILES:
                 turn_x(s)
+            if 4 <= s < 6:
+                table_to_psum(s - 4)
+            if 3 <= s < 5:
+                turn_table(s - 3)
+            if normed(e - 2):
+                rope_sum(e - 2)
             if 1 <= s <= TOK_TILES:
                 quantize_x(s - 1)
+            if s + 1 < UNITS:
+                widen(s + 1, False)
+            if s < UNITS:
+                interleave_b(s)
             if 1 <= s <= UNITS:
                 quantize(s - 1)
+            if s < UNITS:
+                interleave_a(s)
+            if normed(e - 1):
+                rope_products(e - 1)
+            if 0 <= e < TILES:
+                add_bias(e)
+            for u, i in late:
+                multiply(u, i)
+            late.clear()
             if s == PASSES:
                 for i in range(TOK_TILES):
                     for g in range(PASSES):
                         multiply(g, i)
             if PASSES < s <= UNITS:
                 for i in range(TOK_TILES):
-                    multiply(s - 1, i)
-            if 0 <= e < TILES:
-                add_bias(e)
+                    if (s - 1) % PASSES == 0 and i == TOK_TILES - 1:
+                        late.append((s - 1, i))
+                    else:
+                        multiply(s - 1, i)
             if normed(e - 1):
-                invert(e - 1)
-            if s + 1 < UNITS:
-                widen(s + 1, False)
-            if s < UNITS:
-                interleave(s)
-            if normed(e):
-                rope_first(e)
-                mean_square(e)
-            if normed(e - 1):
-                rope_rest(e - 1)
+                mean_square(e - 1)
+            if normed(e - 2):
+                scale_out(e - 2)

@@ -19,19 +19,21 @@ ACT = mybir.ActivationFunctionType
 P = 128
 PACK = 4
 PASSES = C // (P * PACK)
-TOK_TILES = (B * T) // P
+TOKENS = B * T
+TOK_TILES = TOKENS // P
 CHUNK = 512
 HALF = CHUNK // 2
 HEADS = CHUNK // D
+ONES = 64
 
 CHUNKS = (("q", 0), ("q", 1), ("q", 2), ("q", 3), ("k", 0), ("v", 0))
 UNITS = len(CHUNKS) * PASSES
-TILES = len(CHUNKS) * TOK_TILES
-EPI_LAG = 5
+ALL_HEADS = len(CHUNKS) * HEADS
+EPI_LAG = 4
 
-PLANES_ON_SCALAR = (3, 3, 3, 3, 0, 0)
+PLANES_ON_SCALAR = (3, 4, 4, 4, 0, 0)
 A_ON_GPSIMD = (False, True, True, True, True, True)
-B_COLS_ON_SCALAR = (0, 96, 96, 96, 256, 256)
+B_COLS_ON_SCALAR = (0, 0, 0, 0, 256, 256)
 
 
 def tile_llamacausalselfattention_pa_kernel(
@@ -51,9 +53,9 @@ def tile_llamacausalselfattention_pa_kernel(
         wkv = Wk.rearrange("(g p t) n -> g p t n", p=P, t=PACK)
         wvv = Wv.rearrange("(g p t) n -> g p t n", p=P, t=PACK)
         outs = {
-            "q": out_0.rearrange("b t h d -> (b t) (h d)"),
-            "k": out_1.rearrange("b t h d -> (b t) (h d)"),
-            "v": out_2.rearrange("b t h d -> (b t) (h d)"),
+            "q": out_0.rearrange("b t h d -> (b t) (h d)").rearrange("(i p) c -> p i c", p=P),
+            "k": out_1.rearrange("b t h d -> (b t) (h d)").rearrange("(i p) c -> p i c", p=P),
+            "v": out_2.rearrange("b t h d -> (b t) (h d)").rearrange("(i p) c -> p i c", p=P),
         }
 
         wsc = const.tile([P, PASSES, PACK], F32, name="wsc")
@@ -67,16 +69,6 @@ def tile_llamacausalselfattention_pa_kernel(
             gain[kind] = const.tile([P, D], BF16, name="gain_" + kind)
             nc.scalar.dma_start(out=gain[kind][:], in_=vec.partition_broadcast(P))
 
-        bias = const.tile([P, len(CHUNKS) * CHUNK], BF16, name="bias")
-
-        def load_bias(c):
-            kind, cq = CHUNKS[c]
-            vec = {"q": bq, "k": bk, "v": bv}[kind]
-            nc.sync.dma_start(
-                out=bias[:, c * CHUNK : (c + 1) * CHUNK],
-                in_=vec[cq * CHUNK : (cq + 1) * CHUNK].partition_broadcast(P),
-            )
-
         wq8a = []
         wq8b = []
         xraw = []
@@ -85,25 +77,23 @@ def tile_llamacausalselfattention_pa_kernel(
         for g in range(PASSES):
             wq8a.append(raw.tile([P, PACK, CHUNK], U8, name="wq8a%d" % g))
             nc.sync.dma_start(out=wq8a[g][:], in_=wqv[g][:, :, 0:CHUNK])
+        brow = const.tile([P, D], BF16, name="brow")
+        nc.vector.memset(brow[:], 0.0)
+        nc.sync.dma_start(out=brow[0:H, :], in_=bq.rearrange("(h d) -> h d", d=D))
+        nc.sync.dma_start(out=brow[H : H + KV, :], in_=bk.rearrange("(h d) -> h d", d=D))
+        nc.sync.dma_start(out=brow[H + KV : H + 2 * KV, :], in_=bv.rearrange("(h d) -> h d", d=D))
         for i in range(TOK_TILES):
             xraw.append(raw.tile([P, C], BF16, name="xraw%d" % i))
             nc.sync.dma_start(out=xraw[i][:], in_=xv[i * P : (i + 1) * P, :])
-        load_bias(0)
         for g in range(PASSES):
             wq8b.append(raw.tile([P, PACK, 3 * CHUNK], U8, name="wq8b%d" % g))
             nc.sync.dma_start(out=wq8b[g][:], in_=wqv[g][:, :, CHUNK : 4 * CHUNK])
-            if g == 1:
-                load_bias(1)
-        load_bias(2)
-        load_bias(3)
         for g in range(PASSES):
             wkraw.append(raw.tile([P, PACK, CHUNK], BF16, name="wkraw%d" % g))
             nc.sync.dma_start(out=wkraw[g][:], in_=wkv[g])
-        load_bias(4)
         for g in range(PASSES):
             wvraw.append(raw.tile([P, PACK, CHUNK], BF16, name="wvraw%d" % g))
             nc.sync.dma_start(out=wvraw[g][:], in_=wvv[g])
-        load_bias(5)
 
         zero = const.tile([P, 1], F32, name="zero")
         nc.vector.memset(zero[:], 0.0)
@@ -111,8 +101,15 @@ def tile_llamacausalselfattention_pa_kernel(
         nc.vector.tensor_scalar(out=eps[:], in0=zero[:], scalar1=1.0, scalar2=EPS, op0=ALU.mult, op1=ALU.add)
         warm = const.tile([P, 1], F32, name="warm")
         nc.scalar.activation(out=warm[:], in_=eps[:], func=ACT.Abs_reciprocal_sqrt)
+        ones = const.tile([P, ONES], F32, name="ones")
+        nc.vector.memset(ones[:], 1.0)
         ident = const.tile([P, P], F32, name="ident")
         make_identity(nc, ident[:])
+        swap = const.tile([P, P], F32, name="swap")
+        nc.vector.tensor_copy(
+            out=swap[:].rearrange("p (j e) -> p j e", e=2),
+            in_=ident[:].rearrange("p (j e) -> p j e", e=2)[:, :, ::-1],
+        )
 
         ssin = const.tile([P, 2, D // 2, 2], BF16, name="ssin")
         nc.gpsimd.tensor_copy(out=ssin[:, :, :, 0], in_=sin[:])
@@ -137,35 +134,31 @@ def tile_llamacausalselfattention_pa_kernel(
                     op=ALU.mult,
                 )
 
-        table_ps = []
-        table_turned = []
+        bcol = const.tile([P, ALL_HEADS], F32, name="bcol")
+
+        def turn_bias():
+            brow32 = const.tile([P, D], F32, name="brow32")
+            nc.vector.tensor_copy(out=brow32[:], in_=brow[:])
+            bcol_ps = psum.tile([P, P], F32, name="bcol_ps", tag="bank")
+            nc.tensor.transpose(bcol_ps[:], brow32[:], ident[:])
+            nc.vector.tensor_copy(out=bcol[:], in_=bcol_ps[:, 0:ALL_HEADS])
+
+        table = const.tile([P, 2, 2, T], F32, name="table")
 
         def turn_table(i):
             turned_ps = psum.tile([P, 2, 2, D], F32, name="turned_ps", tag="bank")
             for a in range(2):
                 for b in range(2):
                     nc.tensor.transpose(turned_ps[:, a, b, :], table_sb[i][:, a, b, :], ident[:])
-            turned = const.tile([P, 2, 2, D], F32, name="turned%d" % i)
-            table_turned.append(turned)
-            nc.vector.tensor_copy(out=turned[:], in_=turned_ps[:])
-
-        def table_to_psum(i):
-            tab = psum.tile([P, 2, 2, D], F32, name="table_ps%d" % i, tag="table_ps%d" % i, bufs=1)
-            table_ps.append(tab)
-            for a in range(2):
-                for b in range(2):
-                    nc.tensor.transpose(tab[:, a, b, :], table_turned[i][:, a, b, :], ident[:])
+            nc.vector.tensor_copy(out=table[:, :, :, i * P : (i + 1) * P], in_=turned_ps[:])
 
         xgrouped = {}
-        xcodes = []
-        xscales = []
-        for i in range(TOK_TILES):
-            xcodes.append(const.tile([P, PASSES * P], U32, name="xcodes%d" % i, align_bytes=64))
-            xscales.append(const.tile([P, PASSES * P], U8, name="xscales%d" % i, align_bytes=64))
+        xcodes = const.tile([P, PASSES, TOKENS], U32, name="xcodes", align_bytes=64)
+        xscales = const.tile([P, PASSES, TOKENS], U8, name="xscales", align_bytes=64)
 
         def turn_x(i):
             words = xraw[i][:].bitcast(F32)
-            xg = prep.tile([P, PASSES * P * PACK], BF16, name="xg", tag="xg", bufs=2, align_bytes=64)
+            xg = prep.tile([P, PASSES * P * PACK], BF16, name="xg", tag="xg", bufs=4, align_bytes=64)
             xgrouped[i] = xg
             xg_words = xg[:].bitcast(F32).rearrange("p (g r u) -> p g r u", g=PASSES, u=2)
             for half in range(PASSES // 2):
@@ -180,7 +173,12 @@ def tile_llamacausalselfattention_pa_kernel(
                 )
 
         def quantize_x(i):
-            nc.vector.quantize_mx(out=xcodes[i][:].bitcast(FP8X4), scales=xscales[i][:], in_=xgrouped[i][:])
+            for g in range(PASSES):
+                nc.vector.quantize_mx(
+                    out=xcodes[:, g, i * P : (i + 1) * P].bitcast(FP8X4),
+                    scales=xscales[:, g, i * P : (i + 1) * P],
+                    in_=xgrouped[i][:, g * P * PACK : (g + 1) * P * PACK],
+                )
 
         planes = {}
         group_a = {}
@@ -228,8 +226,8 @@ def tile_llamacausalselfattention_pa_kernel(
                 nc.vector.tensor_copy(out=gr[:], in_=turned)
 
         def quantize(u):
-            wcodes[u] = prep.tile([P, CHUNK], U32, name="wcodes", tag="wcodes", bufs=6, align_bytes=64)
-            wscales[u] = prep.tile([P, CHUNK], U8, name="wscales", tag="wscales", bufs=6, align_bytes=64)
+            wcodes[u] = prep.tile([P, CHUNK], U32, name="wcodes", tag="wcodes", bufs=7, align_bytes=64)
+            wscales[u] = prep.tile([P, CHUNK], U8, name="wscales", tag="wscales", bufs=7, align_bytes=64)
             for lo, gr in ((HALF, group_b[u]), (0, group_a[u])):
                 nc.vector.quantize_mx(
                     out=wcodes[u][:, lo : lo + HALF].bitcast(FP8X4),
@@ -239,122 +237,139 @@ def tile_llamacausalselfattention_pa_kernel(
 
         acc = {}
 
-        def multiply(u, i):
+        def multiply(u, hh):
             c, g = divmod(u, PASSES)
-            e = c * TOK_TILES + i
+            e = c * HEADS + hh
             if g == 0:
-                acc[e] = psum.tile([P, CHUNK], F32, name="acc", tag="bank")
+                acc[e] = psum.tile([P, TOKENS], F32, name="acc", tag="bank")
             nc.tensor.matmul_mx(
                 out=acc[e][:],
-                lhsT=xcodes[i][:, g * P : (g + 1) * P].bitcast(FP8X4),
-                lhsT_scale=xscales[i][:, g * P : (g + 1) * P],
-                rhs=wcodes[u][:].bitcast(FP8X4),
-                rhs_scale=wscales[u][:],
+                lhsT=wcodes[u][:, hh * D : (hh + 1) * D].bitcast(FP8X4),
+                lhsT_scale=wscales[u][:, hh * D : (hh + 1) * D],
+                rhs=xcodes[:, g, :].bitcast(FP8X4),
+                rhs_scale=xscales[:, g, :],
                 start=(g == 0),
                 stop=(g == PASSES - 1),
             )
 
-        hb = {}
-        prod = {}
-        rot = {}
+        first = {}
+        second = {}
+        square = {}
+        sums = {}
         rstd = {}
+        back = {}
 
-        def store(e, res):
-            c, i = divmod(e, TOK_TILES)
-            kind, cq = CHUNKS[c]
-            nc.sync.dma_start(out=outs[kind][i * P : (i + 1) * P, cq * CHUNK : (cq + 1) * CHUNK], in_=res[:])
+        def exists(e):
+            return 0 <= e < ALL_HEADS
 
         def normed(e):
-            return 0 <= e < TILES and CHUNKS[e // TOK_TILES][0] != "v"
+            return exists(e) and CHUNKS[e // HEADS][0] != "v"
 
-        def add_bias(e):
-            c = e // TOK_TILES
+        def products(e):
+            kind = CHUNKS[e // HEADS][0]
+            for which, ab in ((first, 0), (second, 1)):
+                name = "first" if ab == 0 else "second"
+                which[e] = epi.tile([P, TOKENS], F32, name=name, tag=name)
+                nc.vector.scalar_tensor_tensor(
+                    out=which[e][:].rearrange("p (b t) -> p b t", b=B),
+                    in0=acc[e][:].rearrange("p (b t) -> p b t", b=B),
+                    scalar=bcol[:, e : e + 1],
+                    in1=table[:, KIND_ROW[kind], ab, :].unsqueeze(1).to_broadcast([P, B, T]),
+                    op0=ALU.add,
+                    op1=ALU.mult,
+                )
+
+        def on_scalar_from_psum(e):
             if normed(e):
-                hb[e] = epi.tile([P, CHUNK], F32, name="hb", tag="hb")
+                square[e] = epi.tile([P, TOKENS], F32, name="square", tag="square")
+                nc.scalar.activation(out=square[e][:], in_=acc[e][:], func=ACT.Square, bias=bcol[:, e : e + 1])
             else:
-                hb[e] = epi.tile([P, CHUNK], F32, name="res", tag="res", bufs=4)
-            nc.vector.tensor_tensor(out=hb[e][:], in0=acc[e][:], in1=bias[:, c * CHUNK : (c + 1) * CHUNK], op=ALU.add)
-            if not normed(e):
-                store(e, hb[e])
+                first[e] = epi.tile([P, TOKENS], F32, name="first", tag="first")
+                nc.scalar.activation(out=first[e][:], in_=acc[e][:], func=ACT.Identity, bias=bcol[:, e : e + 1])
 
-        def mean_square(e):
-            ss = epi.tile([P, HEADS], F32, name="ss", tag="ss", bufs=4)
-            for h in range(HEADS):
-                junk = epi.tile([P, D], F32, name="junk", tag="junk", bufs=2)
-                nc.scalar.activation(out=junk[:], in_=hb[e][:, h * D : (h + 1) * D], func=ACT.Square, accum_out=ss[:, h : h + 1])
-            rstd[e] = epi.tile([P, HEADS], F32, name="rstd", tag="rstd", bufs=4)
-            nc.scalar.activation(out=rstd[e][:], in_=ss[:], func=ACT.Abs_reciprocal_sqrt, bias=eps[:], scale=1.0 / D)
+        def sum_squares(e):
+            sums[e] = psum.tile([P, TOK_TILES, ONES], F32, name="sums", tag="sums", bufs=1)
+            for i in range(TOK_TILES):
+                nc.tensor.matmul(out=sums[e][:, i, :], lhsT=square[e][:, i * P : (i + 1) * P], rhs=ones[:], start=True, stop=True)
 
-        def rope_products(e):
-            c, i = divmod(e, TOK_TILES)
-            tab = table_ps[i % 2][:, KIND_ROW[CHUNKS[c][0]], :, :]
-            prod[e] = epi.tile([P, 2, HEADS, D], F32, name="prod", tag="prod")
-            nc.vector.tensor_tensor(
-                out=prod[e][:],
-                in0=hb[e][:].rearrange("p (h d) -> p h d", h=HEADS).unsqueeze(1).to_broadcast([P, 2, HEADS, D]),
-                in1=tab.unsqueeze(2).to_broadcast([P, 2, HEADS, D]),
-                op=ALU.mult,
-            )
+        def inverse_rms(e):
+            rstd[e] = epi.tile([P, TOK_TILES], F32, name="rstd", tag="rstd", bufs=4)
+            nc.scalar.activation(out=rstd[e][:], in_=sums[e][:, :, 0], func=ACT.Abs_reciprocal_sqrt, bias=eps[:], scale=1.0 / D)
 
-        def rope_sum(e):
-            rot[e] = epi.tile([P, CHUNK], F32, name="rot", tag="rot")
-            nc.vector.tensor_tensor(
-                out=rot[e][:].rearrange("p (j e) -> p j e", e=2),
-                in0=prod[e][:, 0, :, :].rearrange("p h (j e) -> p (h j) e", e=2),
-                in1=prod[e][:, 1, :, :].rearrange("p h (j e) -> p (h j) e", e=2)[:, :, ::-1],
-                op=ALU.add,
-            )
+        def turn_back(e):
+            if normed(e):
+                back[e] = psum.tile([P, TOK_TILES, D], F32, name="back", tag="back", bufs=1)
+            else:
+                back[e] = psum.tile([P, TOK_TILES, D], F32, name="back_v", tag="bank")
+            for i in range(TOK_TILES):
+                cols = slice(i * P, (i + 1) * P)
+                if normed(e):
+                    nc.tensor.matmul(out=back[e][:, i, :], lhsT=first[e][:, cols], rhs=ident[:], is_transpose=True, start=True, stop=False)
+                    nc.tensor.matmul(out=back[e][:, i, :], lhsT=second[e][:, cols], rhs=swap[:], is_transpose=True, start=False, stop=True)
+                else:
+                    nc.tensor.transpose(back[e][:, i, :], first[e][:, cols], ident[:])
 
-        def scale_out(e):
-            res = epi.tile([P, CHUNK], F32, name="res", tag="res", bufs=4)
-            for h in range(HEADS):
-                cols = slice(h * D, (h + 1) * D)
-                nc.scalar.activation(out=res[:, cols], in_=rot[e][:, cols], func=ACT.Copy, scale=rstd[e][:, h : h + 1])
-            store(e, res)
+        def finish(e):
+            kind, cq = CHUNKS[e // HEADS]
+            res = epi.tile([P, TOK_TILES, D], F32, name="res", tag="res", bufs=4)
+            if normed(e):
+                nc.vector.tensor_tensor(
+                    out=res[:], in0=back[e][:], in1=rstd[e][:].unsqueeze(2).to_broadcast([P, TOK_TILES, D]), op=ALU.mult
+                )
+            else:
+                nc.vector.tensor_copy(out=res[:], in_=back[e][:])
+            col = cq * CHUNK + (e % HEADS) * D
+            nc.sync.dma_start(out=outs[kind][:, :, col : col + D], in_=res[:])
 
-        late = []
+        pending = []
         widen(0, True)
         widen(0, False)
-        for s in range(UNITS + EPI_LAG):
+        for s in range(UNITS + EPI_LAG + 2):
             e = s - EPI_LAG
             if s + 1 < UNITS:
                 widen(s + 1, True)
-            if s < TOK_TILES:
-                turn_x(s)
-            if 4 <= s < 6:
-                table_to_psum(s - 4)
-            if 3 <= s < 5:
-                turn_table(s - 3)
-            if normed(e - 2):
-                rope_sum(e - 2)
-            if 1 <= s <= TOK_TILES:
-                quantize_x(s - 1)
+            if s == 0:
+                turn_bias()
+            if 1 <= s <= 2:
+                turn_x(2 * s - 2)
+                turn_x(2 * s - 1)
+            if 2 <= s <= 3:
+                turn_table(s - 2)
             if s + 1 < UNITS:
                 widen(s + 1, False)
             if s < UNITS:
                 interleave_b(s)
+            if 2 <= s <= 3:
+                quantize_x(2 * s - 4)
+                quantize_x(2 * s - 3)
             if 1 <= s <= UNITS:
                 quantize(s - 1)
             if s < UNITS:
                 interleave_a(s)
             if normed(e - 1):
-                rope_products(e - 1)
-            if 0 <= e < TILES:
-                add_bias(e)
-            for u, i in late:
-                multiply(u, i)
-            late.clear()
+                sum_squares(e - 1)
             if s == PASSES:
-                for i in range(TOK_TILES):
+                for hh in range(HEADS):
                     for g in range(PASSES):
-                        multiply(g, i)
+                        multiply(g, hh)
             if PASSES < s <= UNITS:
-                for i in range(TOK_TILES):
-                    if (s - 1) % PASSES == 0 and i == TOK_TILES - 1:
-                        late.append((s - 1, i))
-                    else:
-                        multiply(s - 1, i)
+                c = (s - 1) // PASSES
+                for hh in range(HEADS):
+                    pending.append((PASSES * c + 1 + max(0, hh - 2), s - 1, hh))
+            waiting = []
+            for ready, u, hh in pending:
+                if ready <= s:
+                    multiply(u, hh)
+                else:
+                    waiting.append((ready, u, hh))
+            pending = waiting
+            if exists(e - 2):
+                finish(e - 2)
+            if exists(e - 1):
+                turn_back(e - 1)
+            if normed(e):
+                products(e)
+            if exists(e):
+                on_scalar_from_psum(e)
             if normed(e - 1):
-                mean_square(e - 1)
-            if normed(e - 2):
-                scale_out(e - 2)
+                inverse_rms(e - 1)

@@ -19,21 +19,19 @@ ACT = mybir.ActivationFunctionType
 P = 128
 PACK = 4
 PASSES = C // (P * PACK)
-TOKENS = B * T
-TOK_TILES = TOKENS // P
+TOK_TILES = (B * T) // P
 CHUNK = 512
 HALF = CHUNK // 2
 HEADS = CHUNK // D
-ONES = 64
 
 CHUNKS = (("q", 0), ("q", 1), ("q", 2), ("q", 3), ("k", 0), ("v", 0))
 UNITS = len(CHUNKS) * PASSES
-ALL_HEADS = len(CHUNKS) * HEADS
-EPI_LAG = 4
+TILES = len(CHUNKS) * TOK_TILES
+EPI_LAG = 5
 
-PLANES_ON_SCALAR = (3, 4, 4, 4, 0, 0)
+PLANES_ON_SCALAR = (3, 3, 3, 3, 0, 0)
 A_ON_GPSIMD = (False, True, True, True, True, True)
-B_COLS_ON_SCALAR = (0, 0, 0, 0, 256, 256)
+B_COLS_ON_SCALAR = (0, 96, 96, 96, 256, 256)
 
 
 def tile_llamacausalselfattention_pa_kernel(
@@ -53,9 +51,9 @@ def tile_llamacausalselfattention_pa_kernel(
         wkv = Wk.rearrange("(g p t) n -> g p t n", p=P, t=PACK)
         wvv = Wv.rearrange("(g p t) n -> g p t n", p=P, t=PACK)
         outs = {
-            "q": out_0.rearrange("b t h d -> (b t) (h d)").rearrange("(i p) c -> p i c", p=P),
-            "k": out_1.rearrange("b t h d -> (b t) (h d)").rearrange("(i p) c -> p i c", p=P),
-            "v": out_2.rearrange("b t h d -> (b t) (h d)").rearrange("(i p) c -> p i c", p=P),
+            "q": out_0.rearrange("b t h d -> (b t) (h d)"),
+            "k": out_1.rearrange("b t h d -> (b t) (h d)"),
+            "v": out_2.rearrange("b t h d -> (b t) (h d)"),
         }
 
         wsc = const.tile([P, PASSES, PACK], F32, name="wsc")
@@ -69,6 +67,16 @@ def tile_llamacausalselfattention_pa_kernel(
             gain[kind] = const.tile([P, D], BF16, name="gain_" + kind)
             nc.scalar.dma_start(out=gain[kind][:], in_=vec.partition_broadcast(P))
 
+        bias = const.tile([P, len(CHUNKS) * CHUNK], BF16, name="bias")
+
+        def load_bias(c):
+            kind, cq = CHUNKS[c]
+            vec = {"q": bq, "k": bk, "v": bv}[kind]
+            nc.sync.dma_start(
+                out=bias[:, c * CHUNK : (c + 1) * CHUNK],
+                in_=vec[cq * CHUNK : (cq + 1) * CHUNK].partition_broadcast(P),
+            )
+
         wq8a = []
         wq8b = []
         xraw = []
@@ -77,23 +85,25 @@ def tile_llamacausalselfattention_pa_kernel(
         for g in range(PASSES):
             wq8a.append(raw.tile([P, PACK, CHUNK], U8, name="wq8a%d" % g))
             nc.sync.dma_start(out=wq8a[g][:], in_=wqv[g][:, :, 0:CHUNK])
-        brow = const.tile([P, D], BF16, name="brow")
-        nc.vector.memset(brow[:], 0.0)
-        nc.sync.dma_start(out=brow[0:H, :], in_=bq.rearrange("(h d) -> h d", d=D))
-        nc.sync.dma_start(out=brow[H : H + KV, :], in_=bk.rearrange("(h d) -> h d", d=D))
-        nc.sync.dma_start(out=brow[H + KV : H + 2 * KV, :], in_=bv.rearrange("(h d) -> h d", d=D))
         for i in range(TOK_TILES):
             xraw.append(raw.tile([P, C], BF16, name="xraw%d" % i))
             nc.sync.dma_start(out=xraw[i][:], in_=xv[i * P : (i + 1) * P, :])
+        load_bias(0)
         for g in range(PASSES):
             wq8b.append(raw.tile([P, PACK, 3 * CHUNK], U8, name="wq8b%d" % g))
             nc.sync.dma_start(out=wq8b[g][:], in_=wqv[g][:, :, CHUNK : 4 * CHUNK])
+            if g == 1:
+                load_bias(1)
+        load_bias(2)
+        load_bias(3)
         for g in range(PASSES):
             wkraw.append(raw.tile([P, PACK, CHUNK], BF16, name="wkraw%d" % g))
             nc.sync.dma_start(out=wkraw[g][:], in_=wkv[g])
+        load_bias(4)
         for g in range(PASSES):
             wvraw.append(raw.tile([P, PACK, CHUNK], BF16, name="wvraw%d" % g))
             nc.sync.dma_start(out=wvraw[g][:], in_=wvv[g])
+        load_bias(5)
 
         zero = const.tile([P, 1], F32, name="zero")
         nc.vector.memset(zero[:], 0.0)
@@ -101,15 +111,8 @@ def tile_llamacausalselfattention_pa_kernel(
         nc.vector.tensor_scalar(out=eps[:], in0=zero[:], scalar1=1.0, scalar2=EPS, op0=ALU.mult, op1=ALU.add)
         warm = const.tile([P, 1], F32, name="warm")
         nc.scalar.activation(out=warm[:], in_=eps[:], func=ACT.Abs_reciprocal_sqrt)
-        ones = const.tile([P, ONES], F32, name="ones")
-        nc.vector.memset(ones[:], 1.0)
         ident = const.tile([P, P], F32, name="ident")
         make_identity(nc, ident[:])
-        swap = const.tile([P, P], F32, name="swap")
-        nc.vector.tensor_copy(
-            out=swap[:].rearrange("p (j e) -> p j e", e=2),
-            in_=ident[:].rearrange("p (j e) -> p j e", e=2)[:, :, ::-1],
-        )
 
         ssin = const.tile([P, 2, D // 2, 2], BF16, name="ssin")
         nc.gpsimd.tensor_copy(out=ssin[:, :, :, 0], in_=sin[:])
@@ -134,31 +137,35 @@ def tile_llamacausalselfattention_pa_kernel(
                     op=ALU.mult,
                 )
 
-        bcol = const.tile([P, ALL_HEADS], F32, name="bcol")
-
-        def turn_bias():
-            brow32 = const.tile([P, D], F32, name="brow32")
-            nc.vector.tensor_copy(out=brow32[:], in_=brow[:])
-            bcol_ps = psum.tile([P, P], F32, name="bcol_ps", tag="bank")
-            nc.tensor.transpose(bcol_ps[:], brow32[:], ident[:])
-            nc.vector.tensor_copy(out=bcol[:], in_=bcol_ps[:, 0:ALL_HEADS])
-
-        table = const.tile([P, 2, 2, T], F32, name="table")
+        table_ps = []
+        table_turned = []
 
         def turn_table(i):
             turned_ps = psum.tile([P, 2, 2, D], F32, name="turned_ps", tag="bank")
             for a in range(2):
                 for b in range(2):
                     nc.tensor.transpose(turned_ps[:, a, b, :], table_sb[i][:, a, b, :], ident[:])
-            nc.vector.tensor_copy(out=table[:, :, :, i * P : (i + 1) * P], in_=turned_ps[:])
+            turned = const.tile([P, 2, 2, D], F32, name="turned%d" % i)
+            table_turned.append(turned)
+            nc.vector.tensor_copy(out=turned[:], in_=turned_ps[:])
+
+        def table_to_psum(i):
+            tab = psum.tile([P, 2, 2, D], F32, name="table_ps%d" % i, tag="table_ps%d" % i, bufs=1)
+            table_ps.append(tab)
+            for a in range(2):
+                for b in range(2):
+                    nc.tensor.transpose(tab[:, a, b, :], table_turned[i][:, a, b, :], ident[:])
 
         xgrouped = {}
-        xcodes = const.tile([P, PASSES, TOKENS], U32, name="xcodes", align_bytes=64)
-        xscales = const.tile([P, PASSES, TOKENS], U8, name="xscales", align_bytes=64)
+        xcodes = []
+        xscales = []
+        for i in range(TOK_TILES):
+            xcodes.append(const.tile([P, PASSES * P], U32, name="xcodes%d" % i, align_bytes=64))
+            xscales.append(const.tile([P, PASSES * P], U8, name="xscales%d" % i, align_bytes=64))
 
         def turn_x(i):
             words = xraw[i][:].bitcast(F32)
-            xg = prep.tile([P, PASSES * P * PACK], BF16, name="xg", tag="xg", bufs=4, align_bytes=64)
+            xg = prep.tile([P, PASSES * P * PACK], BF16, name="xg", tag="xg", bufs=2, align_bytes=64)
             xgrouped[i] = xg
             xg_words = xg[:].bitcast(F32).rearrange("p (g r u) -> p g r u", g=PASSES, u=2)
             for half in range(PASSES // 2):
@@ -173,12 +180,7 @@ def tile_llamacausalselfattention_pa_kernel(
                 )
 
         def quantize_x(i):
-            for g in range(PASSES):
-                nc.vector.quantize_mx(
-                    out=xcodes[:, g, i * P : (i + 1) * P].bitcast(FP8X4),
-                    scales=xscales[:, g, i * P : (i + 1) * P],
-                    in_=xgrouped[i][:, g * P * PACK : (g + 1) * P * PACK],
-                )
+            nc.vector.quantize_mx(out=xcodes[i][:].bitcast(FP8X4), scales=xscales[i][:], in_=xgrouped[i][:])
 
         planes = {}
         group_a = {}
@@ -212,22 +214,29 @@ def tile_llamacausalselfattention_pa_kernel(
             gr = prep.tile([P, HALF, PACK], BF16, name="group_b", tag="group_b", align_bytes=64)
             group_b[u] = gr
             if ns > 0:
-                nc.scalar.copy(out=gr[:, 0:ns, :], in_=planes[u][:, :, HALF : HALF + ns].rearrange("p t n -> p n t"))
+                nc.scalar.copy(
+                    out=gr[:, 0:ns, :].rearrange("p (c i) t -> p c t i", i=4),
+                    in_=planes[u][:, :, HALF : HALF + ns].rearrange("p t (c i) -> p c t i", i=4),
+                )
             if ns < HALF:
-                nc.vector.tensor_copy(out=gr[:, ns:HALF, :], in_=planes[u][:, :, HALF + ns : CHUNK].rearrange("p t n -> p n t"))
+                nc.vector.tensor_copy(
+                    out=gr[:, ns:HALF, :].rearrange("p (c i) t -> p c t i", i=4),
+                    in_=planes[u][:, :, HALF + ns : CHUNK].rearrange("p t (c i) -> p c t i", i=4),
+                )
 
         def interleave_a(u):
             gr = prep.tile([P, HALF, PACK], BF16, name="group_a", tag="group_a", bufs=1, align_bytes=64)
             group_a[u] = gr
-            turned = planes[u][:, :, 0:HALF].rearrange("p t n -> p n t")
+            turned = planes[u][:, :, 0:HALF].rearrange("p t (c i) -> p c t i", i=4)
+            target = gr[:].rearrange("p (c i) t -> p c t i", i=4)
             if A_ON_GPSIMD[u // PASSES]:
-                nc.gpsimd.tensor_scalar(out=gr[:], in0=turned, scalar1=1.0, scalar2=0.0, op0=ALU.mult, op1=ALU.add)
+                nc.gpsimd.tensor_scalar(out=target, in0=turned, scalar1=1.0, scalar2=0.0, op0=ALU.mult, op1=ALU.add)
             else:
-                nc.vector.tensor_copy(out=gr[:], in_=turned)
+                nc.vector.tensor_copy(out=target, in_=turned)
 
         def quantize(u):
-            wcodes[u] = prep.tile([P, CHUNK], U32, name="wcodes", tag="wcodes", bufs=7, align_bytes=64)
-            wscales[u] = prep.tile([P, CHUNK], U8, name="wscales", tag="wscales", bufs=7, align_bytes=64)
+            wcodes[u] = prep.tile([P, CHUNK], U32, name="wcodes", tag="wcodes", bufs=6, align_bytes=64)
+            wscales[u] = prep.tile([P, CHUNK], U8, name="wscales", tag="wscales", bufs=6, align_bytes=64)
             for lo, gr in ((HALF, group_b[u]), (0, group_a[u])):
                 nc.vector.quantize_mx(
                     out=wcodes[u][:, lo : lo + HALF].bitcast(FP8X4),
@@ -237,139 +246,122 @@ def tile_llamacausalselfattention_pa_kernel(
 
         acc = {}
 
-        def multiply(u, hh):
+        def multiply(u, i):
             c, g = divmod(u, PASSES)
-            e = c * HEADS + hh
+            e = c * TOK_TILES + i
             if g == 0:
-                acc[e] = psum.tile([P, TOKENS], F32, name="acc", tag="bank")
+                acc[e] = psum.tile([P, CHUNK], F32, name="acc", tag="bank")
             nc.tensor.matmul_mx(
                 out=acc[e][:],
-                lhsT=wcodes[u][:, hh * D : (hh + 1) * D].bitcast(FP8X4),
-                lhsT_scale=wscales[u][:, hh * D : (hh + 1) * D],
-                rhs=xcodes[:, g, :].bitcast(FP8X4),
-                rhs_scale=xscales[:, g, :],
+                lhsT=xcodes[i][:, g * P : (g + 1) * P].bitcast(FP8X4),
+                lhsT_scale=xscales[i][:, g * P : (g + 1) * P],
+                rhs=wcodes[u][:].bitcast(FP8X4),
+                rhs_scale=wscales[u][:],
                 start=(g == 0),
                 stop=(g == PASSES - 1),
             )
 
-        first = {}
-        second = {}
-        square = {}
-        sums = {}
+        hb = {}
+        prod = {}
+        rot = {}
         rstd = {}
-        back = {}
 
-        def exists(e):
-            return 0 <= e < ALL_HEADS
+        def store(e, res):
+            c, i = divmod(e, TOK_TILES)
+            kind, cq = CHUNKS[c]
+            nc.sync.dma_start(out=outs[kind][i * P : (i + 1) * P, cq * CHUNK : (cq + 1) * CHUNK], in_=res[:])
 
         def normed(e):
-            return exists(e) and CHUNKS[e // HEADS][0] != "v"
+            return 0 <= e < TILES and CHUNKS[e // TOK_TILES][0] != "v"
 
-        def products(e):
-            kind = CHUNKS[e // HEADS][0]
-            for which, ab in ((first, 0), (second, 1)):
-                name = "first" if ab == 0 else "second"
-                which[e] = epi.tile([P, TOKENS], F32, name=name, tag=name)
-                nc.vector.scalar_tensor_tensor(
-                    out=which[e][:].rearrange("p (b t) -> p b t", b=B),
-                    in0=acc[e][:].rearrange("p (b t) -> p b t", b=B),
-                    scalar=bcol[:, e : e + 1],
-                    in1=table[:, KIND_ROW[kind], ab, :].unsqueeze(1).to_broadcast([P, B, T]),
-                    op0=ALU.add,
-                    op1=ALU.mult,
-                )
-
-        def on_scalar_from_psum(e):
+        def add_bias(e):
+            c = e // TOK_TILES
             if normed(e):
-                square[e] = epi.tile([P, TOKENS], F32, name="square", tag="square")
-                nc.scalar.activation(out=square[e][:], in_=acc[e][:], func=ACT.Square, bias=bcol[:, e : e + 1])
+                hb[e] = epi.tile([P, CHUNK], F32, name="hb", tag="hb")
             else:
-                first[e] = epi.tile([P, TOKENS], F32, name="first", tag="first")
-                nc.scalar.activation(out=first[e][:], in_=acc[e][:], func=ACT.Identity, bias=bcol[:, e : e + 1])
+                hb[e] = epi.tile([P, CHUNK], F32, name="res", tag="res", bufs=4)
+            nc.vector.tensor_tensor(out=hb[e][:], in0=acc[e][:], in1=bias[:, c * CHUNK : (c + 1) * CHUNK], op=ALU.add)
+            if not normed(e):
+                store(e, hb[e])
 
-        def sum_squares(e):
-            sums[e] = psum.tile([P, TOK_TILES, ONES], F32, name="sums", tag="sums", bufs=1)
-            for i in range(TOK_TILES):
-                nc.tensor.matmul(out=sums[e][:, i, :], lhsT=square[e][:, i * P : (i + 1) * P], rhs=ones[:], start=True, stop=True)
+        def mean_square(e):
+            ss = epi.tile([P, HEADS], F32, name="ss", tag="ss", bufs=4)
+            for h in range(HEADS):
+                junk = epi.tile([P, D], F32, name="junk", tag="junk", bufs=2)
+                nc.scalar.activation(out=junk[:], in_=hb[e][:, h * D : (h + 1) * D], func=ACT.Square, accum_out=ss[:, h : h + 1])
+            rstd[e] = epi.tile([P, HEADS], F32, name="rstd", tag="rstd", bufs=4)
+            nc.scalar.activation(out=rstd[e][:], in_=ss[:], func=ACT.Abs_reciprocal_sqrt, bias=eps[:], scale=1.0 / D)
 
-        def inverse_rms(e):
-            rstd[e] = epi.tile([P, TOK_TILES], F32, name="rstd", tag="rstd", bufs=4)
-            nc.scalar.activation(out=rstd[e][:], in_=sums[e][:, :, 0], func=ACT.Abs_reciprocal_sqrt, bias=eps[:], scale=1.0 / D)
+        def rope_products(e):
+            c, i = divmod(e, TOK_TILES)
+            tab = table_ps[i % 2][:, KIND_ROW[CHUNKS[c][0]], :, :]
+            prod[e] = epi.tile([P, 2, HEADS, D], F32, name="prod", tag="prod")
+            nc.vector.tensor_tensor(
+                out=prod[e][:],
+                in0=hb[e][:].rearrange("p (h d) -> p h d", h=HEADS).unsqueeze(1).to_broadcast([P, 2, HEADS, D]),
+                in1=tab.unsqueeze(2).to_broadcast([P, 2, HEADS, D]),
+                op=ALU.mult,
+            )
 
-        def turn_back(e):
-            if normed(e):
-                back[e] = psum.tile([P, TOK_TILES, D], F32, name="back", tag="back", bufs=1)
-            else:
-                back[e] = psum.tile([P, TOK_TILES, D], F32, name="back_v", tag="bank")
-            for i in range(TOK_TILES):
-                cols = slice(i * P, (i + 1) * P)
-                if normed(e):
-                    nc.tensor.matmul(out=back[e][:, i, :], lhsT=first[e][:, cols], rhs=ident[:], is_transpose=True, start=True, stop=False)
-                    nc.tensor.matmul(out=back[e][:, i, :], lhsT=second[e][:, cols], rhs=swap[:], is_transpose=True, start=False, stop=True)
-                else:
-                    nc.tensor.transpose(back[e][:, i, :], first[e][:, cols], ident[:])
+        def rope_sum(e):
+            rot[e] = epi.tile([P, CHUNK], F32, name="rot", tag="rot")
+            nc.vector.tensor_tensor(
+                out=rot[e][:].rearrange("p (j e) -> p j e", e=2),
+                in0=prod[e][:, 0, :, :].rearrange("p h (j e) -> p (h j) e", e=2),
+                in1=prod[e][:, 1, :, :].rearrange("p h (j e) -> p (h j) e", e=2)[:, :, ::-1],
+                op=ALU.add,
+            )
 
-        def finish(e):
-            kind, cq = CHUNKS[e // HEADS]
-            res = epi.tile([P, TOK_TILES, D], F32, name="res", tag="res", bufs=4)
-            if normed(e):
-                nc.vector.tensor_tensor(
-                    out=res[:], in0=back[e][:], in1=rstd[e][:].unsqueeze(2).to_broadcast([P, TOK_TILES, D]), op=ALU.mult
-                )
-            else:
-                nc.vector.tensor_copy(out=res[:], in_=back[e][:])
-            col = cq * CHUNK + (e % HEADS) * D
-            nc.sync.dma_start(out=outs[kind][:, :, col : col + D], in_=res[:])
+        def scale_out(e):
+            res = epi.tile([P, CHUNK], F32, name="res", tag="res", bufs=4)
+            for h in range(HEADS):
+                cols = slice(h * D, (h + 1) * D)
+                nc.scalar.activation(out=res[:, cols], in_=rot[e][:, cols], func=ACT.Copy, scale=rstd[e][:, h : h + 1])
+            store(e, res)
 
-        pending = []
+        late = []
         widen(0, True)
         widen(0, False)
-        for s in range(UNITS + EPI_LAG + 2):
+        for s in range(UNITS + EPI_LAG):
             e = s - EPI_LAG
             if s + 1 < UNITS:
                 widen(s + 1, True)
-            if s == 0:
-                turn_bias()
-            if 1 <= s <= 2:
-                turn_x(2 * s - 2)
-                turn_x(2 * s - 1)
-            if 2 <= s <= 3:
-                turn_table(s - 2)
+            if s < TOK_TILES:
+                turn_x(s)
+            if 4 <= s < 6:
+                table_to_psum(s - 4)
+            if 3 <= s < 5:
+                turn_table(s - 3)
+            if normed(e - 2):
+                rope_sum(e - 2)
+            if 1 <= s <= TOK_TILES:
+                quantize_x(s - 1)
             if s + 1 < UNITS:
                 widen(s + 1, False)
             if s < UNITS:
                 interleave_b(s)
-            if 2 <= s <= 3:
-                quantize_x(2 * s - 4)
-                quantize_x(2 * s - 3)
             if 1 <= s <= UNITS:
                 quantize(s - 1)
             if s < UNITS:
                 interleave_a(s)
             if normed(e - 1):
-                sum_squares(e - 1)
+                rope_products(e - 1)
+            if 0 <= e < TILES:
+                add_bias(e)
+            for u, i in late:
+                multiply(u, i)
+            late.clear()
             if s == PASSES:
-                for hh in range(HEADS):
+                for i in range(TOK_TILES):
                     for g in range(PASSES):
-                        multiply(g, hh)
+                        multiply(g, i)
             if PASSES < s <= UNITS:
-                c = (s - 1) // PASSES
-                for hh in range(HEADS):
-                    pending.append((PASSES * c + 1 + max(0, hh - 2), s - 1, hh))
-            waiting = []
-            for ready, u, hh in pending:
-                if ready <= s:
-                    multiply(u, hh)
-                else:
-                    waiting.append((ready, u, hh))
-            pending = waiting
-            if exists(e - 2):
-                finish(e - 2)
-            if exists(e - 1):
-                turn_back(e - 1)
-            if normed(e):
-                products(e)
-            if exists(e):
-                on_scalar_from_psum(e)
+                for i in range(TOK_TILES):
+                    if (s - 1) % PASSES == 0 and i == TOK_TILES - 1:
+                        late.append((s - 1, i))
+                    else:
+                        multiply(s - 1, i)
             if normed(e - 1):
-                inverse_rms(e - 1)
+                mean_square(e - 1)
+            if normed(e - 2):
+                scale_out(e - 2)

@@ -237,7 +237,7 @@ def tile_llamacausalselfattention_pa_kernel(
         def quantize(u):
             wcodes[u] = prep.tile([P, CHUNK], U32, name="wcodes", tag="wcodes", bufs=6, align_bytes=64)
             wscales[u] = prep.tile([P, CHUNK], U8, name="wscales", tag="wscales", bufs=6, align_bytes=64)
-            for lo, gr in ((HALF, group_b[u]), (0, group_a[u])):
+            for lo, gr in ((0, group_a[u]), (HALF, group_b[u])):
                 nc.vector.quantize_mx(
                     out=wcodes[u][:, lo : lo + HALF].bitcast(FP8X4),
                     scales=wscales[u][:, lo : lo + HALF],
@@ -279,7 +279,7 @@ def tile_llamacausalselfattention_pa_kernel(
             if normed(e):
                 hb[e] = epi.tile([P, CHUNK], F32, name="hb", tag="hb")
             else:
-                hb[e] = epi.tile([P, CHUNK], F32, name="res", tag="res", bufs=4)
+                hb[e] = epi.tile([P, CHUNK], F32, name="res", tag="res", bufs=8)
             nc.vector.tensor_tensor(out=hb[e][:], in0=acc[e][:], in1=bias[:, c * CHUNK : (c + 1) * CHUNK], op=ALU.add)
             if not normed(e):
                 store(e, hb[e])
@@ -305,7 +305,8 @@ def tile_llamacausalselfattention_pa_kernel(
 
         def rope_sum(e):
             rot[e] = epi.tile([P, CHUNK], F32, name="rot", tag="rot")
-            nc.vector.tensor_tensor(
+            engine = nc.gpsimd if e + EPI_LAG + 2 > UNITS else nc.vector
+            engine.tensor_tensor(
                 out=rot[e][:].rearrange("p (j e) -> p j e", e=2),
                 in0=prod[e][:, 0, :, :].rearrange("p h (j e) -> p (h j) e", e=2),
                 in1=prod[e][:, 1, :, :].rearrange("p h (j e) -> p (h j) e", e=2)[:, :, ::-1],
@@ -313,7 +314,7 @@ def tile_llamacausalselfattention_pa_kernel(
             )
 
         def scale_out(e):
-            res = epi.tile([P, CHUNK], F32, name="res", tag="res", bufs=4)
+            res = epi.tile([P, CHUNK], F32, name="res", tag="res", bufs=8)
             for h in range(HEADS):
                 cols = slice(h * D, (h + 1) * D)
                 nc.scalar.activation(out=res[:, cols], in_=rot[e][:, cols], func=ACT.Copy, scale=rstd[e][:, h : h + 1])

@@ -31,7 +31,7 @@ EPI_LAG = 5
 
 PLANES_ON_SCALAR = (3, 3, 3, 3, 0, 0)
 A_ON_GPSIMD = (False, True, True, True, True, True)
-B_COLS_ON_SCALAR = (0, 96, 96, 96, 256, 256)
+B_COLS_ON_SCALAR = (0, 128, 128, 128, 256, 256)
 
 
 def tile_llamacausalselfattention_pa_kernel(
@@ -138,23 +138,17 @@ def tile_llamacausalselfattention_pa_kernel(
                 )
 
         table_ps = []
-        table_turned = []
-
-        def turn_table(i):
-            turned_ps = psum.tile([P, 2, 2, D], F32, name="turned_ps", tag="bank")
-            for a in range(2):
-                for b in range(2):
-                    nc.tensor.transpose(turned_ps[:, a, b, :], table_sb[i][:, a, b, :], ident[:])
-            turned = const.tile([P, 2, 2, D], F32, name="turned%d" % i)
-            table_turned.append(turned)
-            nc.vector.tensor_copy(out=turned[:], in_=turned_ps[:])
 
         def table_to_psum(i):
             tab = psum.tile([P, 2, 2, D], F32, name="table_ps%d" % i, tag="table_ps%d" % i, bufs=1)
             table_ps.append(tab)
-            for a in range(2):
-                for b in range(2):
-                    nc.tensor.transpose(tab[:, a, b, :], table_turned[i][:, a, b, :], ident[:])
+            nc.tensor.matmul(
+                out=tab[:].rearrange("p a b d -> p (a b d)"),
+                lhsT=ident[:],
+                rhs=table_sb[i][:].rearrange("p a b d -> p (a b d)"),
+                start=True,
+                stop=True,
+            )
 
         xgrouped = {}
         xcodes = []
@@ -331,12 +325,8 @@ def tile_llamacausalselfattention_pa_kernel(
                 turn_x(s)
             if 4 <= s < 6:
                 table_to_psum(s - 4)
-            if 3 <= s < 5:
-                turn_table(s - 3)
             if normed(e - 2):
                 rope_sum(e - 2)
-            if 1 <= s <= TOK_TILES:
-                quantize_x(s - 1)
             if s + 1 < UNITS:
                 widen(s + 1, False)
             if s < UNITS:
@@ -349,6 +339,8 @@ def tile_llamacausalselfattention_pa_kernel(
                 rope_products(e - 1)
             if 0 <= e < TILES:
                 add_bias(e)
+            if 1 <= s <= TOK_TILES:
+                quantize_x(s - 1)
             for u, i in late:
                 multiply(u, i)
             late.clear()

@@ -62,10 +62,10 @@ def tile_llamacausalselfattention_pa_kernel(
         nc.scalar.dma_start(out=cos[:], in_=freqs_cos.rearrange("(i p) j -> p i j", p=P))
         sin = const.tile([P, 2, D // 2], BF16, name="sin")
         nc.scalar.dma_start(out=sin[:], in_=freqs_sin.rearrange("(i p) j -> p i j", p=P))
-        gain = {}
-        for kind, vec in (("q", qn_w), ("k", kn_w)):
-            gain[kind] = const.tile([P, D], BF16, name="gain_" + kind)
-            nc.scalar.dma_start(out=gain[kind][:], in_=vec.partition_broadcast(P))
+        gain_rows = const.tile([P, 2 * D], BF16, name="gain_rows")
+        nc.gpsimd.memset(gain_rows[:], 0.0)
+        nc.scalar.dma_start(out=gain_rows[0:1, 0:D], in_=qn_w.rearrange("(o d) -> o d", o=1))
+        nc.scalar.dma_start(out=gain_rows[0:1, D : 2 * D], in_=kn_w.rearrange("(o d) -> o d", o=1))
 
         bias = const.tile([P, len(CHUNKS) * CHUNK], BF16, name="bias")
 
@@ -114,6 +114,14 @@ def tile_llamacausalselfattention_pa_kernel(
         ident = const.tile([P, P], F32, name="ident")
         make_identity(nc, ident[:])
 
+        ones = const.tile([P, P], BF16, name="ones")
+        nc.gpsimd.memset(ones[:], 1.0)
+        gain_ps = psum.tile([P, 2 * D], F32, name="gain_ps", tag="bank")
+        nc.tensor.matmul(out=gain_ps[:], lhsT=ones[:], rhs=gain_rows[:], start=True, stop=True)
+        gain_all = const.tile([P, 2 * D], BF16, name="gain_all")
+        nc.vector.tensor_copy(out=gain_all[:], in_=gain_ps[:])
+        gain = {"q": gain_all[:, 0:D], "k": gain_all[:, D : 2 * D]}
+
         ssin = const.tile([P, 2, D // 2, 2], BF16, name="ssin")
         nc.gpsimd.tensor_copy(out=ssin[:, :, :, 0], in_=sin[:])
         nc.gpsimd.tensor_scalar(out=ssin[:, :, :, 1], in0=sin[:], scalar1=-1.0, scalar2=0.0, op0=ALU.mult, op1=ALU.add)
@@ -123,7 +131,7 @@ def tile_llamacausalselfattention_pa_kernel(
             tab = const.tile([P, 2, 2, D], F32, name="table_sb%d" % i)
             table_sb.append(tab)
             for kind in ("q", "k"):
-                pairs = gain[kind][:].rearrange("p (j e) -> p j e", e=2)
+                pairs = gain[kind].rearrange("p (j e) -> p j e", e=2)
                 nc.gpsimd.tensor_tensor(
                     out=tab[:, KIND_ROW[kind], 0, :].rearrange("p (j e) -> p j e", e=2),
                     in0=pairs,

@@ -64,6 +64,8 @@ def tile_llamacausalselfattention_pa_kernel(
         nc.scalar.dma_start(out=sin[:], in_=freqs_sin.rearrange("(i p) j -> p i j", p=P))
         gain_rows = const.tile([P, 2 * D], BF16, name="gain_rows")
         nc.gpsimd.memset(gain_rows[:], 0.0)
+        ones = const.tile([P, P], BF16, name="ones")
+        nc.gpsimd.memset(ones[:], 1.0)
         nc.scalar.dma_start(out=gain_rows[0:1, 0:D], in_=qn_w.rearrange("(o d) -> o d", o=1))
         nc.scalar.dma_start(out=gain_rows[0:1, D : 2 * D], in_=kn_w.rearrange("(o d) -> o d", o=1))
 
@@ -114,36 +116,36 @@ def tile_llamacausalselfattention_pa_kernel(
         ident = const.tile([P, P], F32, name="ident")
         make_identity(nc, ident[:])
 
-        ones = const.tile([P, P], BF16, name="ones")
-        nc.gpsimd.memset(ones[:], 1.0)
         gain_ps = psum.tile([P, 2 * D], F32, name="gain_ps", tag="bank")
         nc.tensor.matmul(out=gain_ps[:], lhsT=ones[:], rhs=gain_rows[:], start=True, stop=True)
-        gain_all = const.tile([P, 2 * D], BF16, name="gain_all")
-        nc.vector.tensor_copy(out=gain_all[:], in_=gain_ps[:])
-        gain = {"q": gain_all[:, 0:D], "k": gain_all[:, D : 2 * D]}
 
         ssin = const.tile([P, 2, D // 2, 2], BF16, name="ssin")
         nc.gpsimd.tensor_copy(out=ssin[:, :, :, 0], in_=sin[:])
         nc.gpsimd.tensor_scalar(out=ssin[:, :, :, 1], in0=sin[:], scalar1=-1.0, scalar2=0.0, op0=ALU.mult, op1=ALU.add)
         KIND_ROW = {"q": 0, "k": 1}
         table_sb = []
-        for i in range(2):
-            tab = const.tile([P, 2, 2, D], F32, name="table_sb%d" % i)
-            table_sb.append(tab)
-            for kind in ("q", "k"):
-                pairs = gain[kind].rearrange("p (j e) -> p j e", e=2)
-                nc.gpsimd.tensor_tensor(
-                    out=tab[:, KIND_ROW[kind], 0, :].rearrange("p (j e) -> p j e", e=2),
-                    in0=pairs,
-                    in1=cos[:, i, :].unsqueeze(2).to_broadcast([P, D // 2, 2]),
-                    op=ALU.mult,
-                )
-                nc.gpsimd.tensor_tensor(
-                    out=tab[:, KIND_ROW[kind], 1, :].rearrange("p (j e) -> p j e", e=2),
-                    in0=pairs,
-                    in1=ssin[:, i, :, :],
-                    op=ALU.mult,
-                )
+
+        def build_tables():
+            gain_all = const.tile([P, 2 * D], BF16, name="gain_all")
+            nc.scalar.copy(out=gain_all[:], in_=gain_ps[:])
+            gain = {"q": gain_all[:, 0:D], "k": gain_all[:, D : 2 * D]}
+            for i in range(2):
+                tab = const.tile([P, 2, 2, D], F32, name="table_sb%d" % i)
+                table_sb.append(tab)
+                for kind in ("q", "k"):
+                    pairs = gain[kind].rearrange("p (j e) -> p j e", e=2)
+                    nc.gpsimd.tensor_tensor(
+                        out=tab[:, KIND_ROW[kind], 0, :].rearrange("p (j e) -> p j e", e=2),
+                        in0=pairs,
+                        in1=cos[:, i, :].unsqueeze(2).to_broadcast([P, D // 2, 2]),
+                        op=ALU.mult,
+                    )
+                    nc.gpsimd.tensor_tensor(
+                        out=tab[:, KIND_ROW[kind], 1, :].rearrange("p (j e) -> p j e", e=2),
+                        in0=pairs,
+                        in1=ssin[:, i, :, :],
+                        op=ALU.mult,
+                    )
 
         table_ps = []
 
@@ -329,6 +331,8 @@ def tile_llamacausalselfattention_pa_kernel(
             e = s - EPI_LAG
             if s + 1 < UNITS:
                 widen(s + 1, True)
+            if s == 0:
+                build_tables()
             if s < TOK_TILES:
                 turn_x(s)
             if 4 <= s < 6:

@@ -79,33 +79,33 @@ def tile_llamacausalselfattention_pa_kernel(
                 in_=vec[cq * CHUNK : (cq + 1) * CHUNK].partition_broadcast(P),
             )
 
-        wq8a = []
-        wq8b = []
-        xraw = []
-        wkraw = []
-        wvraw = []
-        for g in range(PASSES):
-            wq8a.append(raw.tile([P, PACK, CHUNK], U8, name="wq8a%d" % g))
-            nc.sync.dma_start(out=wq8a[g][:], in_=wqv[g][:, :, 0:CHUNK])
-        for i in range(TOK_TILES):
-            xraw.append(raw.tile([P, C], BF16, name="xraw%d" % i))
-            nc.sync.dma_start(out=xraw[i][:], in_=xv[i * P : (i + 1) * P, :])
-        load_bias(0)
-        for g in range(PASSES):
-            wq8b.append(raw.tile([P, PACK, 3 * CHUNK], U8, name="wq8b%d" % g))
-            nc.sync.dma_start(out=wq8b[g][:], in_=wqv[g][:, :, CHUNK : 4 * CHUNK])
-            if g == 1:
-                load_bias(1)
-        load_bias(2)
-        load_bias(3)
-        for g in range(PASSES):
-            wkraw.append(raw.tile([P, PACK, CHUNK], BF16, name="wkraw%d" % g))
-            nc.sync.dma_start(out=wkraw[g][:], in_=wkv[g])
-        load_bias(4)
-        for g in range(PASSES):
-            wvraw.append(raw.tile([P, PACK, CHUNK], BF16, name="wvraw%d" % g))
-            nc.sync.dma_start(out=wvraw[g][:], in_=wvv[g])
-        load_bias(5)
+        wq8 = {}
+        xraw = {}
+        wkraw = {}
+        wvraw = {}
+
+        def load_unit(u):
+            c, g = divmod(u, PASSES)
+            kind, cq = CHUNKS[c]
+            if kind == "q":
+                wq8[u] = raw.tile([P, PACK, CHUNK], U8, name="wq8_%d" % u)
+                nc.sync.dma_start(out=wq8[u][:], in_=wqv[g][:, :, cq * CHUNK : (cq + 1) * CHUNK])
+            if kind == "k":
+                wkraw[g] = raw.tile([P, PACK, CHUNK], BF16, name="wkraw%d" % g)
+                nc.sync.dma_start(out=wkraw[g][:], in_=wkv[g])
+            if kind == "v":
+                wvraw[g] = raw.tile([P, PACK, CHUNK], BF16, name="wvraw%d" % g)
+                nc.sync.dma_start(out=wvraw[g][:], in_=wvv[g])
+
+        load_unit(0)
+        for s in range(UNITS + EPI_LAG):
+            if s + 1 < UNITS:
+                load_unit(s + 1)
+            if s < TOK_TILES:
+                xraw[s] = raw.tile([P, C], BF16, name="xraw%d" % s)
+                nc.sync.dma_start(out=xraw[s][:], in_=xv[s * P : (s + 1) * P, :])
+            if (s - EPI_LAG + 1) % TOK_TILES == 0 and 0 <= s - EPI_LAG + 1 < TILES:
+                load_bias((s - EPI_LAG + 1) // TOK_TILES)
 
         zero = const.tile([P, 1], F32, name="zero")
         nc.vector.memset(zero[:], 0.0)
@@ -203,10 +203,8 @@ def tile_llamacausalselfattention_pa_kernel(
                 return
             if u not in planes:
                 planes[u] = prep.tile([P, PACK, CHUNK], BF16, name="wide", tag="wide")
-            src = wq8a[g] if cq == 0 else wq8b[g]
-            lo = 0 if cq == 0 else (cq - 1) * CHUNK
             for t in range(PACK):
-                codes8 = src[:, t, lo : lo + CHUNK].bitcast(FP8)
+                codes8 = wq8[u][:, t, :].bitcast(FP8)
                 scale = wsc[:, g, t : t + 1]
                 if on_scalar and t < PLANES_ON_SCALAR[c]:
                     nc.scalar.activation(out=planes[u][:, t, :], in_=codes8, func=ACT.Copy, scale=scale)

@@ -28,10 +28,14 @@ CHUNKS = (("q", 0), ("q", 1), ("q", 2), ("q", 3), ("k", 0), ("v", 0))
 UNITS = len(CHUNKS) * PASSES
 TILES = len(CHUNKS) * TOK_TILES
 EPI_LAG = 5
+ACC_BANKS = 6
 
-PLANES_ON_SCALAR = (3, 3, 3, 3, 0, 0)
-A_ON_GPSIMD = (False, True, True, True, True, True)
-B_COLS_ON_SCALAR = (0, 128, 128, 128, 256, 256)
+PLANES_ON_SCALAR = (2, 3, 3, 3, 0, 0)
+A_GP_FIRST = 7
+A_COLS_ON_GPSIMD = (0, 256, 256, 256, 192, 192)
+B_COLS_ON_SCALAR = (0, 160, 160, 160, 256, 256)
+SUM_HEADS_ON_GPSIMD = (1, 1, 2, 2, 2, 2)
+SUM_GP_LAST = 17
 
 
 def tile_llamacausalselfattention_pa_kernel(
@@ -44,7 +48,7 @@ def tile_llamacausalselfattention_pa_kernel(
         raw = ctx.enter_context(tc.tile_pool(name="raw", bufs=1))
         prep = ctx.enter_context(tc.tile_pool(name="prep", bufs=3))
         epi = ctx.enter_context(tc.tile_pool(name="epi", bufs=3))
-        psum = ctx.enter_context(tc.psum_pool(name="psum", bufs=6))
+        psum = ctx.enter_context(tc.psum_pool(name="psum", bufs=1))
 
         xv = x.rearrange("b t c -> (b t) c")
         wqv = Wq_bytes.rearrange("(g p t) n -> g p t n", p=P, t=PACK)
@@ -58,10 +62,9 @@ def tile_llamacausalselfattention_pa_kernel(
 
         wsc = const.tile([P, PASSES, PACK], F32, name="wsc")
         nc.scalar.dma_start(out=wsc[:], in_=Wq_scale.rearrange("(g p t) o -> p g (t o)", p=P, t=PACK))
-        cos = const.tile([P, 2, D // 2], BF16, name="cos")
-        nc.scalar.dma_start(out=cos[:], in_=freqs_cos.rearrange("(i p) j -> p i j", p=P))
-        sin = const.tile([P, 2, D // 2], BF16, name="sin")
-        nc.scalar.dma_start(out=sin[:], in_=freqs_sin.rearrange("(i p) j -> p i j", p=P))
+        angles = const.tile([P, 2, 2, D // 2], BF16, name="angles")
+        nc.scalar.dma_start(out=angles[:, :, 0, :], in_=freqs_cos.rearrange("(i p) j -> p i j", p=P))
+        nc.scalar.dma_start(out=angles[:, :, 1, :], in_=freqs_sin.rearrange("(i p) j -> p i j", p=P))
         gain_rows = const.tile([P, 2 * D], BF16, name="gain_rows")
         nc.gpsimd.memset(gain_rows[:], 0.0)
         ones = const.tile([P, P], BF16, name="ones")
@@ -115,50 +118,55 @@ def tile_llamacausalselfattention_pa_kernel(
         nc.scalar.activation(out=warm[:], in_=eps[:], func=ACT.Abs_reciprocal_sqrt)
         ident = const.tile([P, P], F32, name="ident")
         make_identity(nc, ident[:])
+        ident16 = const.tile([P, P], BF16, name="ident16")
+        make_identity(nc, ident16[:])
 
-        gain_ps = psum.tile([P, 2 * D], F32, name="gain_ps", tag="bank")
-        nc.tensor.matmul(out=gain_ps[:], lhsT=ones[:], rhs=gain_rows[:], start=True, stop=True)
-
-        ssin = const.tile([P, 2, D // 2, 2], BF16, name="ssin")
-        nc.gpsimd.tensor_copy(out=ssin[:, :, :, 0], in_=sin[:])
-        nc.gpsimd.tensor_scalar(out=ssin[:, :, :, 1], in0=sin[:], scalar1=-1.0, scalar2=0.0, op0=ALU.mult, op1=ALU.add)
         KIND_ROW = {"q": 0, "k": 1}
-        table_sb = []
+        half = D // 2
+        turned_angles = const.tile([P, 2, P], BF16, name="turned_angles")
+        pick = const.tile([P, 2, 2, D], BF16, name="pick")
+        spread = {}
 
-        def build_tables():
-            gain_all = const.tile([P, 2 * D], BF16, name="gain_all")
-            nc.scalar.copy(out=gain_all[:], in_=gain_ps[:])
-            gain = {"q": gain_all[:, 0:D], "k": gain_all[:, D : 2 * D]}
+        def turn_angles():
+            ps = psum.tile([P, 2, P], BF16, name="angles_ps", tag="tables")
             for i in range(2):
-                tab = const.tile([P, 2, 2, D], F32, name="table_sb%d" % i)
-                table_sb.append(tab)
-                for kind in ("q", "k"):
-                    pairs = gain[kind].rearrange("p (j e) -> p j e", e=2)
-                    nc.gpsimd.tensor_tensor(
-                        out=tab[:, KIND_ROW[kind], 0, :].rearrange("p (j e) -> p j e", e=2),
-                        in0=pairs,
-                        in1=cos[:, i, :].unsqueeze(2).to_broadcast([P, D // 2, 2]),
-                        op=ALU.mult,
-                    )
-                    nc.gpsimd.tensor_tensor(
-                        out=tab[:, KIND_ROW[kind], 1, :].rearrange("p (j e) -> p j e", e=2),
-                        in0=pairs,
-                        in1=ssin[:, i, :, :],
-                        op=ALU.mult,
-                    )
+                nc.tensor.transpose(ps[:, i, :], angles[:, i, :, :].rearrange("p a j -> p (a j)"), ident16[:])
+            nc.scalar.copy(out=turned_angles[:], in_=ps[:])
+            gain_ps = psum.tile([P, 2 * D], F32, name="gain_ps", tag="bank3")
+            nc.tensor.matmul(out=gain_ps[:], lhsT=ones[:], rhs=gain_rows[:], start=True, stop=True)
+            spread[0] = gain_ps
+
+        def place_gains():
+            gain = spread[0][:].rearrange("p (k j e) -> p k j e", k=2, e=2)
+            nc.vector.tensor_tensor(
+                out=pick[:, :, 0, :].rearrange("p k (j e) -> p k j e", e=2),
+                in0=gain,
+                in1=ident16[:, 0:half].unsqueeze(1).unsqueeze(3).to_broadcast([P, 2, half, 2]),
+                op=ALU.mult,
+            )
+            for e, sign in ((0, 1.0), (1, -1.0)):
+                nc.vector.scalar_tensor_tensor(
+                    out=pick[:, :, 1, e:D:2],
+                    in0=gain[:, :, :, e],
+                    scalar=sign,
+                    in1=ident16[:, half:P].unsqueeze(1).to_broadcast([P, 2, half]),
+                    op0=ALU.mult,
+                    op1=ALU.mult,
+                )
 
         table_ps = []
 
-        def table_to_psum(i):
-            tab = psum.tile([P, 2, 2, D], F32, name="table_ps%d" % i, tag="table_ps%d" % i, bufs=1)
+        def make_tables(kind):
+            tab = psum.tile([P, 2, 2, D], F32, name="tables", tag="tables", bufs=1)
             table_ps.append(tab)
-            nc.tensor.matmul(
-                out=tab[:].rearrange("p a b d -> p (a b d)"),
-                lhsT=ident[:],
-                rhs=table_sb[i][:].rearrange("p a b d -> p (a b d)"),
-                start=True,
-                stop=True,
-            )
+            for i in range(2):
+                nc.tensor.matmul(
+                    out=tab[:, i, :, :].rearrange("p b d -> p (b d)"),
+                    lhsT=turned_angles[:, i, :],
+                    rhs=pick[:, KIND_ROW[kind], :, :].rearrange("p b d -> p (b d)"),
+                    start=True,
+                    stop=True,
+                )
 
         xgrouped = {}
         xcodes = []
@@ -173,7 +181,7 @@ def tile_llamacausalselfattention_pa_kernel(
             xgrouped[i] = xg
             xg_words = xg[:].bitcast(F32).rearrange("p (g r u) -> p g r u", g=PASSES, u=2)
             for half in range(PASSES // 2):
-                xt = psum.tile([P, 2, 2, P], F32, name="xt", tag="bank")
+                xt = psum.tile([P, 2, 2, P], F32, name="xt", tag="bank%d" % (4 + half))
                 for gg in range(2):
                     g = 2 * half + gg
                     for u in range(2):
@@ -192,7 +200,7 @@ def tile_llamacausalselfattention_pa_kernel(
         wcodes = {}
         wscales = {}
 
-        def widen(u, on_scalar):
+        def widen(u, on_scalar, slots=range(PACK)):
             c, g = divmod(u, PASSES)
             kind, cq = CHUNKS[c]
             if kind == "k":
@@ -203,7 +211,7 @@ def tile_llamacausalselfattention_pa_kernel(
                 return
             if u not in planes:
                 planes[u] = prep.tile([P, PACK, CHUNK], BF16, name="wide", tag="wide")
-            for t in range(PACK):
+            for t in slots:
                 codes8 = wq8[u][:, t, :].bitcast(FP8)
                 scale = wsc[:, g, t : t + 1]
                 if on_scalar and t < PLANES_ON_SCALAR[c]:
@@ -226,19 +234,39 @@ def tile_llamacausalselfattention_pa_kernel(
                     in_=planes[u][:, :, HALF + ns : CHUNK].rearrange("p t (c i) -> p c t i", i=4),
                 )
 
+        def gp_cols(u):
+            return A_COLS_ON_GPSIMD[u // PASSES] if u >= A_GP_FIRST else 96 if u >= EPI_LAG else 0
+
         def interleave_a(u):
+            ng = gp_cols(u)
             gr = prep.tile([P, HALF, PACK], BF16, name="group_a", tag="group_a", bufs=1, align_bytes=64)
             group_a[u] = gr
-            turned = planes[u][:, :, 0:HALF].rearrange("p t (c i) -> p c t i", i=4)
-            target = gr[:].rearrange("p (c i) t -> p c t i", i=4)
-            if A_ON_GPSIMD[u // PASSES]:
-                nc.gpsimd.tensor_scalar(out=target, in0=turned, scalar1=1.0, scalar2=0.0, op0=ALU.mult, op1=ALU.add)
-            else:
-                nc.vector.tensor_copy(out=target, in_=turned)
+            if ng > 0:
+                nc.gpsimd.tensor_scalar(
+                    out=gr[:, 0:ng, :].rearrange("p (c i) t -> p c t i", i=4),
+                    in0=planes[u][:, :, 0:ng].rearrange("p t (c i) -> p c t i", i=4),
+                    scalar1=1.0,
+                    scalar2=0.0,
+                    op0=ALU.mult,
+                    op1=ALU.add,
+                )
+            if ng < HALF and CHUNKS[u // PASSES][0] == "q":
+                nc.vector.tensor_copy(
+                    out=gr[:, ng:HALF, :].rearrange("p (c i) t -> p c t i", i=4),
+                    in_=planes[u][:, :, ng:HALF].rearrange("p t (c i) -> p c t i", i=4),
+                )
+
+        def interleave_a_scalar(u):
+            ng = gp_cols(u)
+            if ng < HALF and CHUNKS[u // PASSES][0] != "q":
+                nc.scalar.copy(
+                    out=group_a[u][:, ng:HALF, :].rearrange("p (c i) t -> p c t i", i=4),
+                    in_=planes[u][:, :, ng:HALF].rearrange("p t (c i) -> p c t i", i=4),
+                )
 
         def quantize(u):
-            wcodes[u] = prep.tile([P, CHUNK], U32, name="wcodes", tag="wcodes", bufs=6, align_bytes=64)
-            wscales[u] = prep.tile([P, CHUNK], U8, name="wscales", tag="wscales", bufs=6, align_bytes=64)
+            wcodes[u] = prep.tile([P, CHUNK], U32, name="wcodes", tag="wcodes", bufs=8, align_bytes=64)
+            wscales[u] = prep.tile([P, CHUNK], U8, name="wscales", tag="wscales", bufs=8, align_bytes=64)
             for lo, gr in ((0, group_a[u]), (HALF, group_b[u])):
                 nc.vector.quantize_mx(
                     out=wcodes[u][:, lo : lo + HALF].bitcast(FP8X4),
@@ -252,7 +280,7 @@ def tile_llamacausalselfattention_pa_kernel(
             c, g = divmod(u, PASSES)
             e = c * TOK_TILES + i
             if g == 0:
-                acc[e] = psum.tile([P, CHUNK], F32, name="acc", tag="bank")
+                acc[e] = psum.tile([P, CHUNK], F32, name="acc%d" % e, tag="bank%d" % (e % ACC_BANKS))
             nc.tensor.matmul_mx(
                 out=acc[e][:],
                 lhsT=xcodes[i][:, g * P : (g + 1) * P].bitcast(FP8X4),
@@ -263,108 +291,122 @@ def tile_llamacausalselfattention_pa_kernel(
                 stop=(g == PASSES - 1),
             )
 
+        def normed(e):
+            return CHUNKS[e // TOK_TILES][0] != "v"
+
+        def due(s, lag):
+            e = s - EPI_LAG - lag
+            return [e] if 0 <= e < TILES and (lag == 0 or normed(e)) else []
+
         hb = {}
         prod = {}
-        rot = {}
         rstd = {}
 
         def store(e, res):
             c, i = divmod(e, TOK_TILES)
             kind, cq = CHUNKS[c]
-            nc.sync.dma_start(out=outs[kind][i * P : (i + 1) * P, cq * CHUNK : (cq + 1) * CHUNK], in_=res[:])
-
-        def normed(e):
-            return 0 <= e < TILES and CHUNKS[e // TOK_TILES][0] != "v"
+            queue = nc.scalar if e >= TILES - 2 else nc.sync
+            queue.dma_start(out=outs[kind][i * P : (i + 1) * P, cq * CHUNK : (cq + 1) * CHUNK], in_=res[:])
 
         def add_bias(e):
             c = e // TOK_TILES
             if normed(e):
-                hb[e] = epi.tile([P, CHUNK], F32, name="hb", tag="hb")
+                hb[e] = epi.tile([P, CHUNK], F32, name="hb", tag="hb", bufs=6)
             else:
                 hb[e] = epi.tile([P, CHUNK], F32, name="res", tag="res", bufs=8)
             nc.vector.tensor_tensor(out=hb[e][:], in0=acc[e][:], in1=bias[:, c * CHUNK : (c + 1) * CHUNK], op=ALU.add)
             if not normed(e):
                 store(e, hb[e])
 
+        ssq = {}
+
         def mean_square(e):
             ss = epi.tile([P, HEADS], F32, name="ss", tag="ss", bufs=4)
+            ssq[e] = ss
             for h in range(HEADS):
                 junk = epi.tile([P, D], F32, name="junk", tag="junk", bufs=2)
                 nc.scalar.activation(out=junk[:], in_=hb[e][:, h * D : (h + 1) * D], func=ACT.Square, accum_out=ss[:, h : h + 1])
+
+        def inverse_rms(e):
             rstd[e] = epi.tile([P, HEADS], F32, name="rstd", tag="rstd", bufs=4)
-            nc.scalar.activation(out=rstd[e][:], in_=ss[:], func=ACT.Abs_reciprocal_sqrt, bias=eps[:], scale=1.0 / D)
+            nc.scalar.activation(out=rstd[e][:], in_=ssq[e][:], func=ACT.Abs_reciprocal_sqrt, bias=eps[:], scale=1.0 / D)
 
         def rope_products(e):
             c, i = divmod(e, TOK_TILES)
-            tab = table_ps[i % 2][:, KIND_ROW[CHUNKS[c][0]], :, :]
-            prod[e] = epi.tile([P, 2, HEADS, D], F32, name="prod", tag="prod")
-            nc.vector.tensor_tensor(
-                out=prod[e][:],
-                in0=hb[e][:].rearrange("p (h d) -> p h d", h=HEADS).unsqueeze(1).to_broadcast([P, 2, HEADS, D]),
-                in1=tab.unsqueeze(2).to_broadcast([P, 2, HEADS, D]),
-                op=ALU.mult,
-            )
-
-        def rope_sum(e):
-            rot[e] = epi.tile([P, CHUNK], F32, name="rot", tag="rot")
-            engine = nc.gpsimd if e + EPI_LAG + 2 > UNITS else nc.vector
-            engine.tensor_tensor(
-                out=rot[e][:].rearrange("p (j e) -> p j e", e=2),
-                in0=prod[e][:, 0, :, :].rearrange("p h (j e) -> p (h j) e", e=2),
-                in1=prod[e][:, 1, :, :].rearrange("p h (j e) -> p (h j) e", e=2)[:, :, ::-1],
-                op=ALU.add,
-            )
-
-        def scale_out(e):
-            res = epi.tile([P, CHUNK], F32, name="res", tag="res", bufs=8)
+            tab = table_ps[KIND_ROW[CHUNKS[c][0]]][:, i % 2, :, :]
+            prod[e] = epi.tile([P, HEADS, 2, D], F32, name="prod", tag="prod")
             for h in range(HEADS):
-                cols = slice(h * D, (h + 1) * D)
-                nc.scalar.activation(out=res[:, cols], in_=rot[e][:, cols], func=ACT.Copy, scale=rstd[e][:, h : h + 1])
-            store(e, res)
+                nc.vector.scalar_tensor_tensor(
+                    out=prod[e][:, h, :, :],
+                    in0=hb[e][:, h * D : (h + 1) * D].unsqueeze(1).to_broadcast([P, 2, D]),
+                    scalar=rstd[e][:, h : h + 1],
+                    in1=tab,
+                    op0=ALU.mult,
+                    op1=ALU.mult,
+                )
 
-        late = []
+        res_of = {}
+
+        def rope_sum(e, on_gpsimd):
+            ng = HEADS if e >= SUM_GP_LAST else SUM_HEADS_ON_GPSIMD[e // TOK_TILES]
+            if not on_gpsimd:
+                res_of[e] = epi.tile([P, CHUNK], F32, name="res", tag="res", bufs=8)
+            lo, hi = (0, ng) if on_gpsimd else (ng, HEADS)
+            if lo < hi:
+                engine = nc.gpsimd if on_gpsimd else nc.vector
+                engine.tensor_tensor(
+                    out=res_of[e][:, lo * D : hi * D].rearrange("p (h j e) -> p h j e", h=hi - lo, e=2),
+                    in0=prod[e][:, lo:hi, 0, :].rearrange("p h (j e) -> p h j e", e=2),
+                    in1=prod[e][:, lo:hi, 1, :].rearrange("p h (j e) -> p h j e", e=2)[:, :, :, ::-1],
+                    op=ALU.add,
+                )
+            if on_gpsimd:
+                store(e, res_of[e])
+
         widen(0, True)
         widen(0, False)
         for s in range(UNITS + EPI_LAG):
-            e = s - EPI_LAG
             if s + 1 < UNITS:
-                widen(s + 1, True)
-            if s == 0:
-                build_tables()
+                widen(s + 1, True, range(0, 1))
+            for e in due(s, 2):
+                inverse_rms(e)
+            if s + 1 < UNITS:
+                widen(s + 1, True, range(1, PACK))
             if s < TOK_TILES:
                 turn_x(s)
-            if 4 <= s < 6:
-                table_to_psum(s - 4)
-            if normed(e - 2):
-                rope_sum(e - 2)
+            if s == 1:
+                turn_angles()
+            if s == 4:
+                make_tables("q")
+            for e in due(s, 3):
+                rope_sum(e, False)
             if s + 1 < UNITS:
                 widen(s + 1, False)
+            if s == 2:
+                place_gains()
             if s < UNITS:
                 interleave_b(s)
             if 1 <= s <= UNITS:
                 quantize(s - 1)
             if s < UNITS:
                 interleave_a(s)
-            if normed(e - 1):
-                rope_products(e - 1)
-            if 0 <= e < TILES:
+            for e in due(s, 3):
+                rope_sum(e, True)
+            for e in due(s, 2):
+                rope_products(e)
+            for e in due(s, 0):
                 add_bias(e)
             if 1 <= s <= TOK_TILES:
                 quantize_x(s - 1)
-            for u, i in late:
-                multiply(u, i)
-            late.clear()
-            if s == PASSES:
+            for c in range(len(CHUNKS)):
                 for i in range(TOK_TILES):
+                    ready = i + 1 if c == 0 else i + TOK_TILES - ACC_BANKS + 1
                     for g in range(PASSES):
-                        multiply(g, i)
-            if PASSES < s <= UNITS:
-                for i in range(TOK_TILES):
-                    if (s - 1) % PASSES == 0 and i == TOK_TILES - 1:
-                        late.append((s - 1, i))
-                    else:
-                        multiply(s - 1, i)
-            if normed(e - 1):
-                mean_square(e - 1)
-            if normed(e - 2):
-                scale_out(e - 2)
+                        if s == c * PASSES + 1 + max(g, ready):
+                            multiply(c * PASSES + g, i)
+            if s == EPI_LAG + 4 * TOK_TILES + 1:
+                make_tables("k")
+            for e in due(s, 1):
+                mean_square(e)
+            if s < UNITS:
+                interleave_a_scalar(s)

@@ -28,9 +28,14 @@ CHUNKS = (("q", 0), ("q", 1), ("q", 2), ("q", 3), ("k", 0), ("v", 0))
 UNITS = len(CHUNKS) * PASSES
 TILES = len(CHUNKS) * TOK_TILES
 EPI_LAG = 5
+X_LAG = 0
 ACC_BANKS = 6
 
-PLANES_ON_SCALAR = (2, 3, 3, 3, 0, 0)
+PLANES_ON_SCALAR = (3, 3, 3, 3, 0, 0)
+TWO_PLANES_UNTIL = 8
+GAINS_STEP = 5
+TURN_STEP = 4
+TABLE_STEP = 6
 A_GP_FIRST = 7
 A_COLS_ON_GPSIMD = (0, 256, 256, 256, 192, 192)
 B_COLS_ON_SCALAR = (0, 160, 160, 160, 256, 256)
@@ -60,17 +65,22 @@ def tile_llamacausalselfattention_pa_kernel(
             "v": out_2.rearrange("b t h d -> (b t) (h d)"),
         }
 
-        wsc = const.tile([P, PASSES, PACK], F32, name="wsc")
-        nc.scalar.dma_start(out=wsc[:], in_=Wq_scale.rearrange("(g p t) o -> p g (t o)", p=P, t=PACK))
+        wsc = []
+        for g in range(PASSES):
+            wsc.append(const.tile([P, PACK], F32, name="wsc%d" % g))
+        scale_rows = Wq_scale.rearrange("(g p t) o -> g p (t o)", p=P, t=PACK)
+        nc.scalar.dma_start(out=wsc[0][:], in_=scale_rows[0])
         angles = const.tile([P, 2, 2, D // 2], BF16, name="angles")
-        nc.scalar.dma_start(out=angles[:, :, 0, :], in_=freqs_cos.rearrange("(i p) j -> p i j", p=P))
-        nc.scalar.dma_start(out=angles[:, :, 1, :], in_=freqs_sin.rearrange("(i p) j -> p i j", p=P))
         gain_rows = const.tile([P, 2 * D], BF16, name="gain_rows")
         nc.gpsimd.memset(gain_rows[:], 0.0)
         ones = const.tile([P, P], BF16, name="ones")
         nc.gpsimd.memset(ones[:], 1.0)
-        nc.scalar.dma_start(out=gain_rows[0:1, 0:D], in_=qn_w.rearrange("(o d) -> o d", o=1))
-        nc.scalar.dma_start(out=gain_rows[0:1, D : 2 * D], in_=kn_w.rearrange("(o d) -> o d", o=1))
+
+        def load_tables():
+            nc.sync.dma_start(out=angles[:, :, 0, :], in_=freqs_cos.rearrange("(i p) j -> p i j", p=P))
+            nc.sync.dma_start(out=angles[:, :, 1, :], in_=freqs_sin.rearrange("(i p) j -> p i j", p=P))
+            nc.sync.dma_start(out=gain_rows[0:1, 0:D], in_=qn_w.rearrange("(o d) -> o d", o=1))
+            nc.sync.dma_start(out=gain_rows[0:1, D : 2 * D], in_=kn_w.rearrange("(o d) -> o d", o=1))
 
         bias = const.tile([P, len(CHUNKS) * CHUNK], BF16, name="bias")
 
@@ -102,8 +112,12 @@ def tile_llamacausalselfattention_pa_kernel(
 
         load_unit(0)
         for s in range(UNITS + EPI_LAG):
+            if s + 1 < PASSES:
+                nc.sync.dma_start(out=wsc[s + 1][:], in_=scale_rows[s + 1])
             if s + 1 < UNITS:
                 load_unit(s + 1)
+            if s == TOK_TILES:
+                load_tables()
             if s < TOK_TILES:
                 xraw[s] = raw.tile([P, C], BF16, name="xraw%d" % s)
                 nc.sync.dma_start(out=xraw[s][:], in_=xv[s * P : (s + 1) * P, :])
@@ -169,6 +183,7 @@ def tile_llamacausalselfattention_pa_kernel(
                 )
 
         xgrouped = {}
+        xturned = {}
         xcodes = []
         xscales = []
         for i in range(TOK_TILES):
@@ -177,18 +192,22 @@ def tile_llamacausalselfattention_pa_kernel(
 
         def turn_x(i):
             words = xraw[i][:].bitcast(F32)
-            xg = prep.tile([P, PASSES * P * PACK], BF16, name="xg", tag="xg", bufs=2, align_bytes=64)
-            xgrouped[i] = xg
-            xg_words = xg[:].bitcast(F32).rearrange("p (g r u) -> p g r u", g=PASSES, u=2)
             for half in range(PASSES // 2):
                 xt = psum.tile([P, 2, 2, P], F32, name="xt", tag="bank%d" % (4 + half))
+                xturned[i, half] = xt
                 for gg in range(2):
                     g = 2 * half + gg
                     for u in range(2):
                         nc.tensor.transpose(xt[:, gg, u, :], words[:, 256 * g + u : 256 * (g + 1) : 2], ident[:])
+
+        def group_x(i):
+            xg = prep.tile([P, PASSES * P * PACK], BF16, name="xg", tag="xg", bufs=2, align_bytes=64)
+            xgrouped[i] = xg
+            xg_words = xg[:].bitcast(F32).rearrange("p (g r u) -> p g r u", g=PASSES, u=2)
+            for half in range(PASSES // 2):
                 nc.scalar.copy(
                     out=xg_words[:, 2 * half : 2 * half + 2, :, :],
-                    in_=xt[:].rearrange("p g u r -> p g r u"),
+                    in_=xturned[i, half][:].rearrange("p g u r -> p g r u"),
                 )
 
         def quantize_x(i):
@@ -211,12 +230,13 @@ def tile_llamacausalselfattention_pa_kernel(
                 return
             if u not in planes:
                 planes[u] = prep.tile([P, PACK, CHUNK], BF16, name="wide", tag="wide")
+            n_scalar = 2 if u < TWO_PLANES_UNTIL else PLANES_ON_SCALAR[c]
             for t in slots:
                 codes8 = wq8[u][:, t, :].bitcast(FP8)
-                scale = wsc[:, g, t : t + 1]
-                if on_scalar and t < PLANES_ON_SCALAR[c]:
+                scale = wsc[g][:, t : t + 1]
+                if on_scalar and t < n_scalar:
                     nc.scalar.activation(out=planes[u][:, t, :], in_=codes8, func=ACT.Copy, scale=scale)
-                if (not on_scalar) and t >= PLANES_ON_SCALAR[c]:
+                if (not on_scalar) and t >= n_scalar:
                     nc.vector.tensor_scalar(out=planes[u][:, t, :], in0=codes8, scalar1=scale, scalar2=None, op0=ALU.mult)
 
         def interleave_b(u):
@@ -374,15 +394,17 @@ def tile_llamacausalselfattention_pa_kernel(
                 widen(s + 1, True, range(1, PACK))
             if s < TOK_TILES:
                 turn_x(s)
-            if s == 1:
+            if 0 <= s - X_LAG < TOK_TILES:
+                group_x(s - X_LAG)
+            if s == TURN_STEP:
                 turn_angles()
-            if s == 4:
+            if s == TABLE_STEP:
                 make_tables("q")
             for e in due(s, 3):
                 rope_sum(e, False)
             if s + 1 < UNITS:
                 widen(s + 1, False)
-            if s == 2:
+            if s == GAINS_STEP:
                 place_gains()
             if s < UNITS:
                 interleave_b(s)
@@ -396,11 +418,11 @@ def tile_llamacausalselfattention_pa_kernel(
                 rope_products(e)
             for e in due(s, 0):
                 add_bias(e)
-            if 1 <= s <= TOK_TILES:
-                quantize_x(s - 1)
+            if 0 <= s - X_LAG - 1 < TOK_TILES:
+                quantize_x(s - X_LAG - 1)
             for c in range(len(CHUNKS)):
                 for i in range(TOK_TILES):
-                    ready = i + 1 if c == 0 else i + TOK_TILES - ACC_BANKS + 1
+                    ready = i + X_LAG + 1 if c == 0 else i + TOK_TILES - ACC_BANKS + 1
                     for g in range(PASSES):
                         if s == c * PASSES + 1 + max(g, ready):
                             multiply(c * PASSES + g, i)

@@ -28,11 +28,10 @@ CHUNKS = (("q", 0), ("q", 1), ("q", 2), ("q", 3), ("k", 0), ("v", 0))
 UNITS = len(CHUNKS) * PASSES
 TILES = len(CHUNKS) * TOK_TILES
 EPI_LAG = 5
-X_LAG = 0
+X_LAG = 1
 ACC_BANKS = 6
 
-PLANES_ON_SCALAR = (3, 3, 3, 3, 0, 0)
-TWO_PLANES_UNTIL = 8
+PLANES_ON_SCALAR = (3, 2, 3, 3, 0, 0)
 GAINS_STEP = 5
 TURN_STEP = 4
 TABLE_STEP = 6
@@ -120,7 +119,8 @@ def tile_llamacausalselfattention_pa_kernel(
                 load_tables()
             if s < TOK_TILES:
                 xraw[s] = raw.tile([P, C], BF16, name="xraw%d" % s)
-                nc.sync.dma_start(out=xraw[s][:], in_=xv[s * P : (s + 1) * P, :])
+                for lo in (0, C // 2):
+                    nc.sync.dma_start(out=xraw[s][:, lo : lo + C // 2], in_=xv[s * P : (s + 1) * P, lo : lo + C // 2])
             if (s - EPI_LAG + 1) % TOK_TILES == 0 and 0 <= s - EPI_LAG + 1 < TILES:
                 load_bias((s - EPI_LAG + 1) // TOK_TILES)
 
@@ -193,7 +193,7 @@ def tile_llamacausalselfattention_pa_kernel(
         def turn_x(i):
             words = xraw[i][:].bitcast(F32)
             for half in range(PASSES // 2):
-                xt = psum.tile([P, 2, 2, P], F32, name="xt", tag="bank%d" % (4 + half))
+                xt = psum.tile([P, 2, 2, P], F32, name="xt", tag="bank%d" % (2 + 2 * (i % 2) + half))
                 xturned[i, half] = xt
                 for gg in range(2):
                     g = 2 * half + gg
@@ -230,7 +230,7 @@ def tile_llamacausalselfattention_pa_kernel(
                 return
             if u not in planes:
                 planes[u] = prep.tile([P, PACK, CHUNK], BF16, name="wide", tag="wide")
-            n_scalar = 2 if u < TWO_PLANES_UNTIL else PLANES_ON_SCALAR[c]
+            n_scalar = 2 if u == 0 else PLANES_ON_SCALAR[c]
             for t in slots:
                 codes8 = wq8[u][:, t, :].bitcast(FP8)
                 scale = wsc[g][:, t : t + 1]
@@ -322,11 +322,11 @@ def tile_llamacausalselfattention_pa_kernel(
         prod = {}
         rstd = {}
 
-        def store(e, res):
+        def store(e, res, cols=slice(0, CHUNK)):
             c, i = divmod(e, TOK_TILES)
             kind, cq = CHUNKS[c]
             queue = nc.scalar if e >= TILES - 2 else nc.sync
-            queue.dma_start(out=outs[kind][i * P : (i + 1) * P, cq * CHUNK : (cq + 1) * CHUNK], in_=res[:])
+            queue.dma_start(out=outs[kind][i * P : (i + 1) * P, cq * CHUNK + cols.start : cq * CHUNK + cols.stop], in_=res[:, cols])
 
         def add_bias(e):
             c = e // TOK_TILES
@@ -334,9 +334,14 @@ def tile_llamacausalselfattention_pa_kernel(
                 hb[e] = epi.tile([P, CHUNK], F32, name="hb", tag="hb", bufs=6)
             else:
                 hb[e] = epi.tile([P, CHUNK], F32, name="res", tag="res", bufs=8)
-            nc.vector.tensor_tensor(out=hb[e][:], in0=acc[e][:], in1=bias[:, c * CHUNK : (c + 1) * CHUNK], op=ALU.add)
-            if not normed(e):
-                store(e, hb[e])
+            pieces = 2 if e == TILES - 1 else 1
+            for n in range(pieces):
+                cols = slice(n * CHUNK // pieces, (n + 1) * CHUNK // pieces)
+                nc.vector.tensor_tensor(
+                    out=hb[e][:, cols], in0=acc[e][:, cols], in1=bias[:, c * CHUNK + cols.start : c * CHUNK + cols.stop], op=ALU.add
+                )
+                if not normed(e):
+                    store(e, hb[e], cols)
 
         ssq = {}
 

@@ -37,7 +37,8 @@ TURN_STEP = 4
 TABLE_STEP = 6
 A_GP_FIRST = 7
 A_COLS_ON_GPSIMD = (0, 256, 256, 256, 192, 192)
-B_COLS_ON_SCALAR = (0, 160, 160, 160, 256, 256)
+B_COLS_ON_TENSOR = (0, 128, 256, 256, 128, 128)
+B_COLS_ON_SCALAR = (0, 0, 0, 0, 128, 128)
 SUM_HEADS_ON_GPSIMD = (1, 1, 2, 2, 2, 2)
 SUM_GP_LAST = 17
 
@@ -239,14 +240,37 @@ def tile_llamacausalselfattention_pa_kernel(
                 if (not on_scalar) and t >= n_scalar:
                     nc.vector.tensor_scalar(out=planes[u][:, t, :], in0=codes8, scalar1=scale, scalar2=None, op0=ALU.mult)
 
+        woven = {}
+
+        def weave(u):
+            nt = B_COLS_ON_TENSOR[u // PASSES]
+            if nt == 0:
+                return
+            woven[u] = psum.tile([P, HALF * PACK], BF16, name="woven", tag="woven", bufs=1)
+            for lo in range(0, nt, P):
+                nc.tensor.matmul(
+                    out=woven[u][:, lo * PACK : (lo + P) * PACK].rearrange("p (n t) -> p n t", t=PACK),
+                    lhsT=ident16[:],
+                    rhs=planes[u][:, :, HALF + lo : HALF + lo + P].rearrange("p t n -> p n t"),
+                    start=True,
+                    stop=True,
+                )
+
+        def unweave(u):
+            nt = B_COLS_ON_TENSOR[u // PASSES]
+            if nt > 0:
+                nc.scalar.copy(out=group_b[u][:, 0:nt, :].rearrange("p n t -> p (n t)"), in_=woven[u][:, 0 : nt * PACK])
+
         def interleave_b(u):
             ns = B_COLS_ON_SCALAR[u // PASSES]
             gr = prep.tile([P, HALF, PACK], BF16, name="group_b", tag="group_b", align_bytes=64)
             group_b[u] = gr
-            if ns > 0:
+            nt = B_COLS_ON_TENSOR[u // PASSES]
+            ns = ns + nt
+            if ns > nt:
                 nc.scalar.copy(
-                    out=gr[:, 0:ns, :].rearrange("p (c i) t -> p c t i", i=4),
-                    in_=planes[u][:, :, HALF : HALF + ns].rearrange("p t (c i) -> p c t i", i=4),
+                    out=gr[:, nt:ns, :].rearrange("p (c i) t -> p c t i", i=4),
+                    in_=planes[u][:, :, HALF + nt : HALF + ns].rearrange("p t (c i) -> p c t i", i=4),
                 )
             if ns < HALF:
                 nc.vector.tensor_copy(
@@ -412,6 +436,7 @@ def tile_llamacausalselfattention_pa_kernel(
             if s == GAINS_STEP:
                 place_gains()
             if s < UNITS:
+                weave(s)
                 interleave_b(s)
             if 1 <= s <= UNITS:
                 quantize(s - 1)
@@ -437,3 +462,4 @@ def tile_llamacausalselfattention_pa_kernel(
                 mean_square(e)
             if s < UNITS:
                 interleave_a_scalar(s)
+                unweave(s)

@@ -36,10 +36,10 @@ GAINS_STEP = 5
 TURN_STEP = 4
 TABLE_STEP = 6
 A_GP_FIRST = 7
-A_COLS_ON_GPSIMD = (0, 256, 256, 256, 192, 192)
+A_COLS_ON_GPSIMD = (0, 256, 256, 256, 128, 128)
 B_COLS_ON_TENSOR = (0, 128, 256, 256, 128, 128)
 B_COLS_ON_SCALAR = (0, 0, 0, 0, 128, 128)
-SUM_HEADS_ON_GPSIMD = (1, 1, 2, 2, 2, 2)
+SUM_HEADS_ON_GPSIMD = (1, 1, 3, 3, 3, 3)
 SUM_GP_LAST = 17
 
 

@@ -37,8 +37,8 @@ TURN_STEP = 4
 TABLE_STEP = 6
 A_GP_FIRST = 7
 A_COLS_ON_GPSIMD = (0, 256, 256, 256, 128, 128)
-B_COLS_ON_TENSOR = (0, 128, 256, 256, 128, 128)
-B_COLS_ON_SCALAR = (0, 0, 0, 0, 128, 128)
+B_COLS_ON_TENSOR = (0, 0, 256, 256, 128, 128)
+B_COLS_ON_SCALAR = (0, 160, 0, 0, 128, 128)
 SUM_HEADS_ON_GPSIMD = (1, 1, 3, 3, 3, 3)
 SUM_GP_LAST = 17
 

from contextlib import ExitStack

import concourse.mybir as mybir
from concourse.masks import make_identity

B, T, C, H, KV, D = 2, 256, 2048, 16, 4, 128
EPS = 1e-5
FLOPS = 2 * (B * T) * C * (H + 2 * KV) * D

F32 = mybir.dt.float32
BF16 = mybir.dt.bfloat16
U32 = mybir.dt.uint32
U8 = mybir.dt.uint8
FP8 = mybir.dt.float8_e4m3fn
FP8X4 = mybir.dt.float8_e4m3fn_x4
ALU = mybir.AluOpType
ACT = mybir.ActivationFunctionType

P = 128
PACK = 4
PASSES = C // (P * PACK)
TOK_TILES = (B * T) // P
CHUNK = 512
HALF = CHUNK // 2
HEADS = CHUNK // D

CHUNKS = (("q", 0), ("q", 1), ("q", 2), ("q", 3), ("k", 0), ("v", 0))
UNITS = len(CHUNKS) * PASSES
TILES = len(CHUNKS) * TOK_TILES
EPI_LAG = 5
X_LAG = 1
ACC_BANKS = 6

PLANES_ON_SCALAR = (3, 2, 3, 3, 0, 0)
GAINS_STEP = 5
TURN_STEP = 4
TABLE_STEP = 6
A_GP_FIRST = 7
A_COLS_ON_GPSIMD = (0, 256, 256, 256, 128, 128)
B_COLS_ON_TENSOR = (0, 0, 256, 256, 128, 128)
B_COLS_ON_SCALAR = (0, 160, 0, 0, 128, 128)
SUM_HEADS_ON_GPSIMD = (1, 1, 3, 3, 3, 3)
SUM_GP_LAST = 17


def tile_llamacausalselfattention_pa_kernel(
    tc, x, Wq_bytes, Wq_scale, bq, Wk, bk, Wv, bv, qn_w, kn_w, freqs_cos, freqs_sin, out_0, out_1, out_2
):
    nc = tc.nc
    with ExitStack() as ctx:
        ctx.enter_context(tc.manual_schedule())
        const = ctx.enter_context(tc.tile_pool(name="const", bufs=1))
        raw = ctx.enter_context(tc.tile_pool(name="raw", bufs=1))
        prep = ctx.enter_context(tc.tile_pool(name="prep", bufs=3))
        epi = ctx.enter_context(tc.tile_pool(name="epi", bufs=3))
        psum = ctx.enter_context(tc.psum_pool(name="psum", bufs=1))

        xv = x.rearrange("b t c -> (b t) c")
        wqv = Wq_bytes.rearrange("(g p t) n -> g p t n", p=P, t=PACK)
        wkv = Wk.rearrange("(g p t) n -> g p t n", p=P, t=PACK)
        wvv = Wv.rearrange("(g p t) n -> g p t n", p=P, t=PACK)
        outs = {
            "q": out_0.rearrange("b t h d -> (b t) (h d)"),
            "k": out_1.rearrange("b t h d -> (b t) (h d)"),
            "v": out_2.rearrange("b t h d -> (b t) (h d)"),
        }

        wsc = []
        for g in range(PASSES):
            wsc.append(const.tile([P, PACK], F32, name="wsc%d" % g))
        scale_rows = Wq_scale.rearrange("(g p t) o -> g p (t o)", p=P, t=PACK)
        nc.scalar.dma_start(out=wsc[0][:], in_=scale_rows[0])
        angles = const.tile([P, 2, 2, D // 2], BF16, name="angles")
        gain_rows = const.tile([P, 2 * D], BF16, name="gain_rows")
        nc.gpsimd.memset(gain_rows[:], 0.0)
        ones = const.tile([P, P], BF16, name="ones")
        nc.gpsimd.memset(ones[:], 1.0)

        def load_tables():
            nc.sync.dma_start(out=angles[:, :, 0, :], in_=freqs_cos.rearrange("(i p) j -> p i j", p=P))
            nc.sync.dma_start(out=angles[:, :, 1, :], in_=freqs_sin.rearrange("(i p) j -> p i j", p=P))
            nc.sync.dma_start(out=gain_rows[0:1, 0:D], in_=qn_w.rearrange("(o d) -> o d", o=1))
            nc.sync.dma_start(out=gain_rows[0:1, D : 2 * D], in_=kn_w.rearrange("(o d) -> o d", o=1))

        bias = const.tile([P, len(CHUNKS) * CHUNK], BF16, name="bias")

        def load_bias(c):
            kind, cq = CHUNKS[c]
            vec = {"q": bq, "k": bk, "v": bv}[kind]
            nc.sync.dma_start(
                out=bias[:, c * CHUNK : (c + 1) * CHUNK],
                in_=vec[cq * CHUNK : (cq + 1) * CHUNK].partition_broadcast(P),
            )

        wq8 = {}
        xraw = {}
        wkraw = {}
        wvraw = {}

        def load_unit(u):
            c, g = divmod(u, PASSES)
            kind, cq = CHUNKS[c]
            if kind == "q":
                wq8[u] = raw.tile([P, PACK, CHUNK], U8, name="wq8_%d" % u)
                nc.sync.dma_start(out=wq8[u][:], in_=wqv[g][:, :, cq * CHUNK : (cq + 1) * CHUNK])
            if kind == "k":
                wkraw[g] = raw.tile([P, PACK, CHUNK], BF16, name="wkraw%d" % g)
                nc.sync.dma_start(out=wkraw[g][:], in_=wkv[g])
            if kind == "v":
                wvraw[g] = raw.tile([P, PACK, CHUNK], BF16, name="wvraw%d" % g)
                nc.sync.dma_start(out=wvraw[g][:], in_=wvv[g])

        load_unit(0)
        for s in range(UNITS + EPI_LAG):
            if s + 1 < PASSES:
                nc.sync.dma_start(out=wsc[s + 1][:], in_=scale_rows[s + 1])
            if s + 1 < UNITS:
                load_unit(s + 1)
            if s == TOK_TILES:
                load_tables()
            if s < TOK_TILES:
                xraw[s] = raw.tile([P, C], BF16, name="xraw%d" % s)
                for lo in (0, C // 2):
                    nc.sync.dma_start(out=xraw[s][:, lo : lo + C // 2], in_=xv[s * P : (s + 1) * P, lo : lo + C // 2])
            if (s - EPI_LAG + 1) % TOK_TILES == 0 and 0 <= s - EPI_LAG + 1 < TILES:
                load_bias((s - EPI_LAG + 1) // TOK_TILES)

        zero = const.tile([P, 1], F32, name="zero")
        nc.vector.memset(zero[:], 0.0)
        eps = const.tile([P, 1], F32, name="eps")
        nc.vector.tensor_scalar(out=eps[:], in0=zero[:], scalar1=1.0, scalar2=EPS, op0=ALU.mult, op1=ALU.add)
        warm = const.tile([P, 1], F32, name="warm")
        nc.scalar.activation(out=warm[:], in_=eps[:], func=ACT.Abs_reciprocal_sqrt)
        ident = const.tile([P, P], F32, name="ident")
        make_identity(nc, ident[:])
        ident16 = const.tile([P, P], BF16, name="ident16")
        make_identity(nc, ident16[:])

        KIND_ROW = {"q": 0, "k": 1}
        half = D // 2
        turned_angles = const.tile([P, 2, P], BF16, name="turned_angles")
        pick = const.tile([P, 2, 2, D], BF16, name="pick")
        spread = {}

        def turn_angles():
            ps = psum.tile([P, 2, P], BF16, name="angles_ps", tag="tables")
            for i in range(2):
                nc.tensor.transpose(ps[:, i, :], angles[:, i, :, :].rearrange("p a j -> p (a j)"), ident16[:])
            nc.scalar.copy(out=turned_angles[:], in_=ps[:])
            gain_ps = psum.tile([P, 2 * D], F32, name="gain_ps", tag="bank3")
            nc.tensor.matmul(out=gain_ps[:], lhsT=ones[:], rhs=gain_rows[:], start=True, stop=True)
            spread[0] = gain_ps

        def place_gains():
            gain = spread[0][:].rearrange("p (k j e) -> p k j e", k=2, e=2)
            nc.vector.tensor_tensor(
                out=pick[:, :, 0, :].rearrange("p k (j e) -> p k j e", e=2),
                in0=gain,
                in1=ident16[:, 0:half].unsqueeze(1).unsqueeze(3).to_broadcast([P, 2, half, 2]),
                op=ALU.mult,
            )
            for e, sign in ((0, 1.0), (1, -1.0)):
                nc.vector.scalar_tensor_tensor(
                    out=pick[:, :, 1, e:D:2],
                    in0=gain[:, :, :, e],
                    scalar=sign,
                    in1=ident16[:, half:P].unsqueeze(1).to_broadcast([P, 2, half]),
                    op0=ALU.mult,
                    op1=ALU.mult,
                )

        table_ps = []

        def make_tables(kind):
            tab = psum.tile([P, 2, 2, D], F32, name="tables", tag="tables", bufs=1)
            table_ps.append(tab)
            for i in range(2):
                nc.tensor.matmul(
                    out=tab[:, i, :, :].rearrange("p b d -> p (b d)"),
                    lhsT=turned_angles[:, i, :],
                    rhs=pick[:, KIND_ROW[kind], :, :].rearrange("p b d -> p (b d)"),
                    start=True,
                    stop=True,
                )

        xgrouped = {}
        xturned = {}
        xcodes = []
        xscales = []
        for i in range(TOK_TILES):
            xcodes.append(const.tile([P, PASSES * P], U32, name="xcodes%d" % i, align_bytes=64))
            xscales.append(const.tile([P, PASSES * P], U8, name="xscales%d" % i, align_bytes=64))

        def turn_x(i):
            words = xraw[i][:].bitcast(F32)
            for half in range(PASSES // 2):
                xt = psum.tile([P, 2, 2, P], F32, name="xt", tag="bank%d" % (2 + 2 * (i % 2) + half))
                xturned[i, half] = xt
                for gg in range(2):
                    g = 2 * half + gg
                    for u in range(2):
                        nc.tensor.transpose(xt[:, gg, u, :], words[:, 256 * g + u : 256 * (g + 1) : 2], ident[:])

        def group_x(i):
            xg = prep.tile([P, PASSES * P * PACK], BF16, name="xg", tag="xg", bufs=2, align_bytes=64)
            xgrouped[i] = xg
            xg_words = xg[:].bitcast(F32).rearrange("p (g r u) -> p g r u", g=PASSES, u=2)
            for half in range(PASSES // 2):
                nc.scalar.copy(
                    out=xg_words[:, 2 * half : 2 * half + 2, :, :],
                    in_=xturned[i, half][:].rearrange("p g u r -> p g r u"),
                )

        def quantize_x(i):
            nc.vector.quantize_mx(out=xcodes[i][:].bitcast(FP8X4), scales=xscales[i][:], in_=xgrouped[i][:])

        planes = {}
        group_a = {}
        group_b = {}
        wcodes = {}
        wscales = {}

        def widen(u, on_scalar, slots=range(PACK)):
            c, g = divmod(u, PASSES)
            kind, cq = CHUNKS[c]
            if kind == "k":
                planes[u] = wkraw[g]
            if kind == "v":
                planes[u] = wvraw[g]
            if kind != "q":
                return
            if u not in planes:
                planes[u] = prep.tile([P, PACK, CHUNK], BF16, name="wide", tag="wide")
            n_scalar = 2 if u == 0 else PLANES_ON_SCALAR[c]
            for t in slots:
                codes8 = wq8[u][:, t, :].bitcast(FP8)
                scale = wsc[g][:, t : t + 1]
                if on_scalar and t < n_scalar:
                    nc.scalar.activation(out=planes[u][:, t, :], in_=codes8, func=ACT.Copy, scale=scale)
                if (not on_scalar) and t >= n_scalar:
                    nc.vector.tensor_scalar(out=planes[u][:, t, :], in0=codes8, scalar1=scale, scalar2=None, op0=ALU.mult)

        woven = {}

        def weave(u):
            nt = B_COLS_ON_TENSOR[u // PASSES]
            if nt == 0:
                return
            woven[u] = psum.tile([P, HALF * PACK], BF16, name="woven", tag="woven", bufs=1)
            for lo in range(0, nt, P):
                nc.tensor.matmul(
                    out=woven[u][:, lo * PACK : (lo + P) * PACK].rearrange("p (n t) -> p n t", t=PACK),
                    lhsT=ident16[:],
                    rhs=planes[u][:, :, HALF + lo : HALF + lo + P].rearrange("p t n -> p n t"),
                    start=True,
                    stop=True,
                )

        def unweave(u):
            nt = B_COLS_ON_TENSOR[u // PASSES]
            if nt > 0:
                nc.scalar.copy(out=group_b[u][:, 0:nt, :].rearrange("p n t -> p (n t)"), in_=woven[u][:, 0 : nt * PACK])

        def interleave_b(u):
            ns = B_COLS_ON_SCALAR[u // PASSES]
            gr = prep.tile([P, HALF, PACK], BF16, name="group_b", tag="group_b", align_bytes=64)
            group_b[u] = gr
            nt = B_COLS_ON_TENSOR[u // PASSES]
            ns = ns + nt
            if ns > nt:
                nc.scalar.copy(
                    out=gr[:, nt:ns, :].rearrange("p (c i) t -> p c t i", i=4),
                    in_=planes[u][:, :, HALF + nt : HALF + ns].rearrange("p t (c i) -> p c t i", i=4),
                )
            if ns < HALF:
                nc.vector.tensor_copy(
                    out=gr[:, ns:HALF, :].rearrange("p (c i) t -> p c t i", i=4),
                    in_=planes[u][:, :, HALF + ns : CHUNK].rearrange("p t (c i) -> p c t i", i=4),
                )

        def gp_cols(u):
            return A_COLS_ON_GPSIMD[u // PASSES] if u >= A_GP_FIRST else 96 if u >= EPI_LAG else 0

        def interleave_a(u):
            ng = gp_cols(u)
            gr = prep.tile([P, HALF, PACK], BF16, name="group_a", tag="group_a", bufs=1, align_bytes=64)
            group_a[u] = gr
            if ng > 0:
                nc.gpsimd.tensor_scalar(
                    out=gr[:, 0:ng, :].rearrange("p (c i) t -> p c t i", i=4),
                    in0=planes[u][:, :, 0:ng].rearrange("p t (c i) -> p c t i", i=4),
                    scalar1=1.0,
                    scalar2=0.0,
                    op0=ALU.mult,
                    op1=ALU.add,
                )
            if ng < HALF and CHUNKS[u // PASSES][0] == "q":
                nc.vector.tensor_copy(
                    out=gr[:, ng:HALF, :].rearrange("p (c i) t -> p c t i", i=4),
                    in_=planes[u][:, :, ng:HALF].rearrange("p t (c i) -> p c t i", i=4),
                )

        def interleave_a_scalar(u):
            ng = gp_cols(u)
            if ng < HALF and CHUNKS[u // PASSES][0] != "q":
                nc.scalar.copy(
                    out=group_a[u][:, ng:HALF, :].rearrange("p (c i) t -> p c t i", i=4),
                    in_=planes[u][:, :, ng:HALF].rearrange("p t (c i) -> p c t i", i=4),
                )

        def quantize(u):
            wcodes[u] = prep.tile([P, CHUNK], U32, name="wcodes", tag="wcodes", bufs=8, align_bytes=64)
            wscales[u] = prep.tile([P, CHUNK], U8, name="wscales", tag="wscales", bufs=8, align_bytes=64)
            for lo, gr in ((0, group_a[u]), (HALF, group_b[u])):
                nc.vector.quantize_mx(
                    out=wcodes[u][:, lo : lo + HALF].bitcast(FP8X4),
                    scales=wscales[u][:, lo : lo + HALF],
                    in_=gr[:].rearrange("p n t -> p (n t)"),
                )

        acc = {}

        def multiply(u, i):
            c, g = divmod(u, PASSES)
            e = c * TOK_TILES + i
            if g == 0:
                acc[e] = psum.tile([P, CHUNK], F32, name="acc%d" % e, tag="bank%d" % (e % ACC_BANKS))
            nc.tensor.matmul_mx(
                out=acc[e][:],
                lhsT=xcodes[i][:, g * P : (g + 1) * P].bitcast(FP8X4),
                lhsT_scale=xscales[i][:, g * P : (g + 1) * P],
                rhs=wcodes[u][:].bitcast(FP8X4),
                rhs_scale=wscales[u][:],
                start=(g == 0),
                stop=(g == PASSES - 1),
            )

        def normed(e):
            return CHUNKS[e // TOK_TILES][0] != "v"

        def due(s, lag):
            e = s - EPI_LAG - lag
            return [e] if 0 <= e < TILES and (lag == 0 or normed(e)) else []

        hb = {}
        prod = {}
        rstd = {}

        def store(e, res, cols=slice(0, CHUNK)):
            c, i = divmod(e, TOK_TILES)
            kind, cq = CHUNKS[c]
            queue = nc.scalar if e >= TILES - 2 else nc.sync
            queue.dma_start(out=outs[kind][i * P : (i + 1) * P, cq * CHUNK + cols.start : cq * CHUNK + cols.stop], in_=res[:, cols])

        def add_bias(e):
            c = e // TOK_TILES
            if normed(e):
                hb[e] = epi.tile([P, CHUNK], F32, name="hb", tag="hb", bufs=6)
            else:
                hb[e] = epi.tile([P, CHUNK], F32, name="res", tag="res", bufs=8)
            pieces = 2 if e == TILES - 1 else 1
            for n in range(pieces):
                cols = slice(n * CHUNK // pieces, (n + 1) * CHUNK // pieces)
                nc.vector.tensor_tensor(
                    out=hb[e][:, cols], in0=acc[e][:, cols], in1=bias[:, c * CHUNK + cols.start : c * CHUNK + cols.stop], op=ALU.add
                )
                if not normed(e):
                    store(e, hb[e], cols)

        ssq = {}

        def mean_square(e):
            ss = epi.tile([P, HEADS], F32, name="ss", tag="ss", bufs=4)
            ssq[e] = ss
            for h in range(HEADS):
                junk = epi.tile([P, D], F32, name="junk", tag="junk", bufs=2)
                nc.scalar.activation(out=junk[:], in_=hb[e][:, h * D : (h + 1) * D], func=ACT.Square, accum_out=ss[:, h : h + 1])

        def inverse_rms(e):
            rstd[e] = epi.tile([P, HEADS], F32, name="rstd", tag="rstd", bufs=4)
            nc.scalar.activation(out=rstd[e][:], in_=ssq[e][:], func=ACT.Abs_reciprocal_sqrt, bias=eps[:], scale=1.0 / D)

        def rope_products(e):
            c, i = divmod(e, TOK_TILES)
            tab = table_ps[KIND_ROW[CHUNKS[c][0]]][:, i % 2, :, :]
            prod[e] = epi.tile([P, HEADS, 2, D], F32, name="prod", tag="prod")
            for h in range(HEADS):
                nc.vector.scalar_tensor_tensor(
                    out=prod[e][:, h, :, :],
                    in0=hb[e][:, h * D : (h + 1) * D].unsqueeze(1).to_broadcast([P, 2, D]),
                    scalar=rstd[e][:, h : h + 1],
                    in1=tab,
                    op0=ALU.mult,
                    op1=ALU.mult,
                )

        res_of = {}

        def rope_sum(e, on_gpsimd):
            ng = HEADS if e >= SUM_GP_LAST else SUM_HEADS_ON_GPSIMD[e // TOK_TILES]
            if not on_gpsimd:
                res_of[e] = epi.tile([P, CHUNK], F32, name="res", tag="res", bufs=8)
            lo, hi = (0, ng) if on_gpsimd else (ng, HEADS)
            if lo < hi:
                engine = nc.gpsimd if on_gpsimd else nc.vector
                engine.tensor_tensor(
                    out=res_of[e][:, lo * D : hi * D].rearrange("p (h j e) -> p h j e", h=hi - lo, e=2),
                    in0=prod[e][:, lo:hi, 0, :].rearrange("p h (j e) -> p h j e", e=2),
                    in1=prod[e][:, lo:hi, 1, :].rearrange("p h (j e) -> p h j e", e=2)[:, :, :, ::-1],
                    op=ALU.add,
                )
            if on_gpsimd:
                store(e, res_of[e])

        widen(0, True)
        widen(0, False)
        for s in range(UNITS + EPI_LAG):
            if s + 1 < UNITS:
                widen(s + 1, True, range(0, 1))
            for e in due(s, 2):
                inverse_rms(e)
            if s + 1 < UNITS:
                widen(s + 1, True, range(1, PACK))
            if s < TOK_TILES:
                turn_x(s)
            if 0 <= s - X_LAG < TOK_TILES:
                group_x(s - X_LAG)
            if s == TURN_STEP:
                turn_angles()
            if s == TABLE_STEP:
                make_tables("q")
            for e in due(s, 3):
                rope_sum(e, False)
            if s + 1 < UNITS:
                widen(s + 1, False)
            if s == GAINS_STEP:
                place_gains()
            if s < UNITS:
                weave(s)
                interleave_b(s)
            if 1 <= s <= UNITS:
                quantize(s - 1)
            if s < UNITS:
                interleave_a(s)
            for e in due(s, 3):
                rope_sum(e, True)
            for e in due(s, 2):
                rope_products(e)
            for e in due(s, 0):
                add_bias(e)
            if 0 <= s - X_LAG - 1 < TOK_TILES:
                quantize_x(s - X_LAG - 1)
            for c in range(len(CHUNKS)):
                for i in range(TOK_TILES):
                    ready = i + X_LAG + 1 if c == 0 else i + TOK_TILES - ACC_BANKS + 1
                    for g in range(PASSES):
                        if s == c * PASSES + 1 + max(g, ready):
                            multiply(c * PASSES + g, i)
            if s == EPI_LAG + 4 * TOK_TILES + 1:
                make_tables("k")
            for e in due(s, 1):
                mean_square(e)
            if s < UNITS:
                interleave_a_scalar(s)
                unweave(s)
